import numpy as np
import ml_dtypes


def mxq(x, axis, fmt="e4m3"):
    dtype, down = {"e4m3": (ml_dtypes.float8_e4m3fn, 7), "e5m2": (ml_dtypes.float8_e5m2, 14)}[fmt]
    v = np.moveaxis(np.asarray(x, np.float32).astype(ml_dtypes.bfloat16).astype(np.float64), axis, -1)
    blocks = v.reshape(v.shape[:-1] + (-1, 32))
    amax = np.abs(blocks).max(-1, keepdims=True)
    byte = np.maximum(np.where(amax > 0, np.frexp(amax)[1] - 1 + 127, 0) - down, 1)
    scale = np.exp2(byte - 127.0)
    codes = (blocks / scale).astype(np.float32).astype(dtype).astype(np.float64)
    return np.moveaxis((codes * scale).reshape(v.shape), -1, axis)


WIDE = False


def mx_kscale(k):
    if not WIDE:
        return np.ones(k)
    levels = np.array([10, -10, 5, -5, 0])
    a = np.random.permutation(np.resize(levels, k // 512 * 4)).reshape(k // 512, 4)
    idx = np.arange(k)
    return np.exp2(a[idx // 512, idx % 128 // 32])


BF16 = ml_dtypes.bfloat16


def bf(x):
    return np.asarray(x, np.float32).astype(BF16)


def f64(x):
    return np.asarray(x).astype(np.float64)


B, S, T, DIM, H = 8, 512, 512, 512, 4
D = DIM // H


def split_heads(t):
    return t.reshape(B, S, H, D).transpose(0, 2, 1, 3)


def setup_inputs():
    s = mx_kscale(DIM)
    return {
        "q": bf(np.random.standard_normal((B, H, S, D)) * 1.4),
        "k_cache": bf(np.random.standard_normal((B, H, T, D)) * 1.4),
        "k_new": bf(np.random.standard_normal((B, H, S, D)) * 1.4),
        "x": bf(np.random.standard_normal((B, S, DIM)) * s),
        "Wv": bf(np.random.standard_normal((DIM, DIM)) / np.sqrt(DIM) / s[None, :]),
        "bv": bf(np.random.standard_normal(DIM) * 0.2),
        "v_cache": bf(np.random.standard_normal((B, H, T, D))),
    }


def reference(q, k_cache, k_new, x, Wv, bv, v_cache):
    v_new = split_heads((mxq(f64(x), 2, "e4m3") @ mxq(f64(Wv), 1, "e4m3").T) + f64(bv))
    v = np.concatenate([f64(v_cache), v_new], axis=2)
    qf = f64(q)
    s = np.concatenate([qf @ f64(k_cache).transpose(0, 1, 3, 2), qf @ f64(k_new).transpose(0, 1, 3, 2)], axis=3) * (1.0 / np.sqrt(D))
    mask = np.arange(T + S)[None, :] <= np.arange(S)[:, None] + T
    s = np.where(mask[None, None], s, -np.inf)
    e = np.exp(s - s.max(-1, keepdims=True))
    ctx = (mxq(e, 3, "e4m3") @ mxq(v, 2, "e4m3")) / e.sum(-1, keepdims=True)
    return ctx.transpose(0, 2, 1, 3).reshape(B, S, DIM), v_new

@@ -1,0 +1,315 @@
+import math
+from contextlib import ExitStack
+
+import concourse.mybir as mybir
+from concourse.masks import make_identity
+
+F32 = mybir.dt.float32
+BF16 = mybir.dt.bfloat16
+U32 = mybir.dt.uint32
+U8 = mybir.dt.uint8
+FP8X4 = mybir.dt.float8_e4m3fn_x4
+ALU = mybir.AluOpType
+ACT = mybir.ActivationFunctionType
+AXIS = mybir.AxisListType
+
+P = 128
+PACK = 4
+B, H, S, T, DIM = 8, 4, 512, 512, 512
+D = DIM // H
+TILES = S // P
+STEPS = B * H * TILES
+STEPS_PER_BATCH = H * TILES
+SCALE = 1.0 / math.sqrt(D)
+MASKED = -1.0e30
+
+FLOPS = 2 * B * H * S * (T + S) * D * 2 + 2 * B * S * DIM * DIM
+
+PREPARE_AHEAD = 6
+SCORES_AHEAD = 2
+MAX_AHEAD = 1
+TRANSPOSE_BEHIND = 1
+QUANTISE_BEHIND = 2
+ATTEND_BEHIND = 3
+FINISH_BEHIND = 4
+VALUES_AHEAD = 10
+VECTOR_COPY_PERIOD = 3
+
+
+def tile_attentionlayer_pa_t_kernel(tc, q, k_cache, k_new, x, Wv, bv, v_cache, out_0, out_1):
+    nc = tc.nc
+    with ExitStack() as stack:
+        const = stack.enter_context(tc.tile_pool(name="const", bufs=1))
+        loads = stack.enter_context(tc.tile_pool(name="loads", bufs=3))
+        heads = stack.enter_context(tc.tile_pool(name="heads", bufs=3))
+        small = stack.enter_context(tc.tile_pool(name="small", bufs=6))
+        work = stack.enter_context(tc.tile_pool(name="work", bufs=3))
+        values = stack.enter_context(tc.tile_pool(name="values", bufs=2))
+        psum_scores = stack.enter_context(tc.psum_pool(name="psum_scores", bufs=4))
+        psum_turn = stack.enter_context(tc.psum_pool(name="psum_turn", bufs=3))
+        psum_ctx = stack.enter_context(tc.psum_pool(name="psum_ctx", bufs=1))
+
+        q_sb, kc_sb, kn_sb, x_sb, vc_sb = {}, {}, {}, {}, {}
+
+        def load_batch(b):
+            x_t = loads.tile([P, TILES, DIM], BF16, tag="x")
+            nc.sync.dma_start(out=x_t[:].rearrange("p (u e) f -> p u (e f)", e=2), in_=x[b].rearrange("(u p e) f -> p u (e f)", p=P, e=2))
+            q_t = loads.tile([P, H * TILES, D], BF16, tag="q")
+            nc.sync.dma_start(out=q_t[:], in_=q[b].rearrange("h (i p) d -> p (h i) d", p=P))
+            kc_t = loads.tile([P, H * TILES, D], BF16, tag="kc")
+            nc.sync.dma_start(out=kc_t[:], in_=k_cache[b].rearrange("h (t p) d -> p (h t) d", p=P))
+            kn_t = loads.tile([P, H * TILES, D], BF16, tag="kn")
+            nc.sync.dma_start(out=kn_t[:], in_=k_new[b].rearrange("h (t p) d -> p (h t) d", p=P))
+            vc_t = loads.tile([P, H, PACK * D], BF16, tag="vc")
+            nc.sync.dma_start(out=vc_t[:].rearrange("p h (u r) -> p (h u) r", u=2), in_=v_cache[b].rearrange("h (u p e) d -> p (h u) (e d)", p=P, e=2))
+            x_sb[b], q_sb[b], kc_sb[b], kn_sb[b], vc_sb[b] = x_t, q_t, kc_t, kn_t, vc_t
+
+        w_sb = const.tile([P, TILES, DIM], BF16)
+        nc.sync.dma_start(out=w_sb[:], in_=Wv.rearrange("(r p) k -> p r k", p=P))
+        load_batch(0)
+        bias_bf = const.tile([P, DIM], BF16)
+        nc.sync.dma_start(out=bias_bf[:], in_=bv.partition_broadcast(P))
+        load_batch(1)
+
+        ident_bf = const.tile([P, P], BF16)
+        make_identity(nc, ident_bf[:])
+        ident_f32 = const.tile([P, P], F32)
+        make_identity(nc, ident_f32[:])
+        mask_f32 = const.tile([P, P], F32)
+        nc.gpsimd.memset(mask_f32[:], 0.0)
+        nc.gpsimd.affine_select(
+            out=mask_f32[:], in_=mask_f32[:], compare_op=ALU.is_ge, fill=MASKED,
+            base=0, pattern=[[-1, P]], channel_multiplier=1,
+        )
+        mask_bf = const.tile([P, P], BF16)
+        nc.vector.tensor_copy(out=mask_bf[:], in_=mask_f32[:])
+        bias = const.tile([P, DIM], F32)
+        nc.vector.tensor_copy(out=bias[:], in_=bias_bf[:])
+        e_sb = []
+        for i in range(TILES):
+            e_t = const.tile([P, T + S], BF16, name="e%d" % i)
+            if i + 1 < TILES:
+                nc.vector.memset(e_t[:, T + (i + 1) * P :], 0.0)
+            e_sb.append(e_t)
+
+        def turn_words(rows, grouped):
+            for pair in range(2):
+                planes = psum_turn.tile([P, 4, P], F32, tag="turn")
+                for r in range(2):
+                    words = rows[:, 2 * pair + r, :].bitcast(F32)
+                    for u in range(2):
+                        nc.tensor.transpose(out=planes[:, 2 * r + u, :], in_=words[:, u * P : (u + 1) * P], identity=ident_f32[:])
+                half = grouped[:, pair * 2 * P * PACK : (pair + 1) * 2 * P * PACK].bitcast(F32)
+                copy = nc.scalar.copy if pair == 0 else nc.vector.tensor_copy
+                copy(
+                    out=half.rearrange("p (r c u) -> p r c u", r=2, u=2),
+                    in_=planes[:].rearrange("p (r u) c -> p r c u", u=2),
+                )
+
+        w_grouped = const.tile([P, DIM * PACK], BF16, align_bytes=64)
+        turn_words(w_sb, w_grouped)
+        w_codes = const.tile([P, DIM], U32, align_bytes=64)
+        w_scales = const.tile([P, DIM], U8, align_bytes=64)
+        nc.vector.quantize_mx(out=w_codes[:].bitcast(FP8X4), scales=w_scales[:], in_=w_grouped[:])
+
+        x_grouped, x_codes, x_scales, v_new, v_grouped, v_codes, v_scales = {}, {}, {}, {}, {}, {}, {}
+
+        def regroup(grouped, rows):
+            nc.gpsimd.tensor_scalar(
+                out=grouped[:].rearrange("p (h d t) -> p h d t", h=H, t=PACK),
+                in0=rows, scalar1=1.0, scalar2=0.0, op0=ALU.mult, op1=ALU.add,
+            )
+
+        def turn_x(b):
+            xg = values.tile([P, S * PACK], BF16, tag="xg", align_bytes=64)
+            turn_words(x_sb[b], xg)
+            x_grouped[b] = xg
+            vg_cache = values.tile([P, DIM * PACK], BF16, tag="vg_cache", align_bytes=64)
+            regroup(vg_cache, vc_sb[b][:].rearrange("p h (t d) -> p h d t", t=PACK))
+            v_grouped[b] = [vg_cache]
+
+        def quantise_x(b):
+            xc = values.tile([P, S], U32, tag="xc", align_bytes=64)
+            xs = values.tile([P, S], U8, tag="xs", align_bytes=64)
+            nc.vector.quantize_mx(out=xc[:].bitcast(FP8X4), scales=xs[:], in_=x_grouped[b][:])
+            x_codes[b], x_scales[b] = xc, xs
+            vn = values.tile([P, H, TILES, D], F32, tag="vn")
+            v_new[b] = vn
+
+        def project(b, t):
+            cols = slice(t * P, (t + 1) * P)
+            acc = psum_turn.tile([P, DIM], F32, tag="turn")
+            nc.tensor.matmul_mx(
+                out=acc[:],
+                lhsT=x_codes[b][:, cols].bitcast(FP8X4), lhsT_scale=x_scales[b][:, cols],
+                rhs=w_codes[:].bitcast(FP8X4), rhs_scale=w_scales[:],
+                start=True, stop=True,
+            )
+            nc.vector.tensor_tensor(
+                out=v_new[b][:, :, t, :],
+                in0=acc[:].rearrange("p (h d) -> p h d", h=H),
+                in1=bias[:].rearrange("p (h d) -> p h d", h=H),
+                op=ALU.add,
+            )
+
+        def regroup_v_new(b):
+            nc.sync.dma_start(out=out_1[b].rearrange("h (u p e) d -> p (h u) (e d)", p=P, e=2), in_=v_new[b][:].rearrange("p h (u e) d -> p (h u) (e d)", e=2))
+            vg_new = values.tile([P, DIM * PACK], BF16, tag="vg_new", align_bytes=64)
+            regroup(vg_new, v_new[b][:].rearrange("p h t d -> p h d t"))
+            v_grouped[b].append(vg_new)
+
+        def quantise_v(b):
+            v_codes[b], v_scales[b] = [], []
+            for g in range(2):
+                vc = values.tile([P, DIM], U32, tag="vc%d" % g, align_bytes=64)
+                vs = values.tile([P, DIM], U8, tag="vs%d" % g, align_bytes=64)
+                nc.vector.quantize_mx(out=vc[:].bitcast(FP8X4), scales=vs[:], in_=v_grouped[b][g][:])
+                v_codes[b].append(vc)
+                v_scales[b].append(vs)
+
+        def prepare_values(b, step):
+            if step == 0:
+                turn_x(b)
+            elif step == 1:
+                quantise_x(b)
+            elif step < 2 + TILES:
+                project(b, step - 2)
+            elif step == 2 + TILES:
+                regroup_v_new(b)
+            elif step == 4 + TILES:
+                quantise_v(b)
+
+        turned, dT, score_banks, neg_max, row_sums, e_turned, e_grouped, e_codes, e_scales, ctx_acc = (
+            {}, {}, {}, {}, {}, {}, {}, {}, {}, {},
+        )
+
+        def prepare_transposes(n):
+            head, r = divmod(n, TILES)
+            b, h = divmod(head, H)
+            blocks = psum_turn.tile([P, 3, P], BF16, tag="turn")
+            nc.tensor.transpose(out=blocks[:, 0, :], in_=q_sb[b][:, h * TILES + r, :], identity=ident_bf[:])
+            nc.tensor.transpose(out=blocks[:, 1, :], in_=kc_sb[b][:, h * TILES + r, :], identity=ident_bf[:])
+            nc.tensor.transpose(out=blocks[:, 2, :], in_=kn_sb[b][:, h * TILES + r, :], identity=ident_bf[:])
+            turned[n] = blocks
+
+        def prepare_copy(n):
+            head, r = divmod(n, TILES)
+            if r == 0:
+                qkT = heads.tile([P, 3, S], BF16, tag="qkT")
+                dT[head] = qkT
+            nc.scalar.copy(out=dT[head][:, :, r * P : (r + 1) * P], in_=turned[n][:])
+
+        def scores(n):
+            head, i = divmod(n, TILES)
+            qT = dT[head][:, 0, i * P : (i + 1) * P]
+            seen = (i + 1) * P
+            cache = psum_scores.tile([P, T], F32, tag="scores")
+            nc.tensor.matmul(out=cache[:], lhsT=qT, rhs=dT[head][:, 1, :], start=True, stop=True)
+            new = psum_scores.tile([P, S], F32, tag="scores")
+            nc.tensor.matmul(out=new[:, :seen], lhsT=qT, rhs=dT[head][:, 2, :seen], start=True, stop=False)
+            nc.tensor.matmul(out=new[:, i * P : seen], lhsT=ident_bf[:], rhs=mask_bf[:], start=False, stop=True)
+            score_banks[n] = [cache[:], new[:, :seen]]
+
+        def row_max(n):
+            both = small.tile([P, 2], F32, tag="both")
+            for g in range(2):
+                nc.vector.tensor_reduce(out=both[:, g : g + 1], in_=score_banks[n][g], axis=AXIS.X, op=ALU.max)
+            nm = small.tile([P, 1], F32, tag="nm")
+            nc.vector.tensor_scalar(
+                out=nm[:], in0=both[:, 0:1], scalar1=both[:, 1:2], scalar2=-SCALE, op0=ALU.max, op1=ALU.mult
+            )
+            neg_max[n] = nm
+
+        def exponentials(n):
+            head, i = divmod(n, TILES)
+            if i == 0:
+                sums = small.tile([P, TILES, 2], F32, tag="sums")
+                row_sums[head] = sums
+            seen = (i + 1) * P
+            for g, cols in enumerate([slice(0, T), slice(T, T + seen)]):
+                nc.scalar.activation(
+                    out=e_sb[i][:, cols], in_=score_banks[n][g], func=ACT.Exp,
+                    bias=neg_max[n][:], scale=SCALE, accum_out=row_sums[head][:, i, g : g + 1],
+                )
+
+        def transpose_e(n):
+            i = n % TILES
+            blocks = psum_turn.tile([P, PACK, P], F32, tag="turn")
+            words = e_sb[i][:].bitcast(F32)
+            for t in range(PACK):
+                nc.tensor.transpose(out=blocks[:, t, :], in_=words[:, t * P : (t + 1) * P], identity=ident_f32[:])
+            e_turned[n] = blocks
+
+        def copy_e(n):
+            eg = work.tile([P, 2 * P * PACK], BF16, tag="eg", align_bytes=64)
+            copy = nc.vector.tensor_copy if n % VECTOR_COPY_PERIOD == 0 else nc.scalar.copy
+            copy(
+                out=eg[:].bitcast(F32).rearrange("p (g c u) -> p g c u", g=2, u=2),
+                in_=e_turned[n][:].rearrange("p (g u) c -> p g c u", g=2),
+            )
+            e_grouped[n] = eg
+
+        def quantise_e(n):
+            ec = work.tile([P, 2 * P], U32, tag="ec", align_bytes=64)
+            es = work.tile([P, 2 * P], U8, tag="es", align_bytes=64)
+            nc.vector.quantize_mx(out=ec[:].bitcast(FP8X4), scales=es[:], in_=e_grouped[n][:])
+            e_codes[n], e_scales[n] = ec, es
+
+        def attend(n):
+            head, i = divmod(n, TILES)
+            b, h = divmod(head, H)
+            if i == 0:
+                acc = psum_ctx.tile([P, TILES, D], F32, tag="ctx")
+                ctx_acc[head] = acc
+            for g in range(2):
+                nc.tensor.matmul_mx(
+                    out=ctx_acc[head][:, i, :],
+                    lhsT=e_codes[n][:, g * P : (g + 1) * P].bitcast(FP8X4),
+                    lhsT_scale=e_scales[n][:, g * P : (g + 1) * P],
+                    rhs=v_codes[b][g][:, h * D : (h + 1) * D].bitcast(FP8X4),
+                    rhs_scale=v_scales[b][g][:, h * D : (h + 1) * D],
+                    start=(g == 0), stop=(g == 1),
+                )
+
+        def finish_head(head):
+            b, h = divmod(head, H)
+            total = small.tile([P, TILES], F32, tag="total")
+            nc.vector.tensor_reduce(out=total[:], in_=row_sums[head][:], axis=AXIS.X, op=ALU.add)
+            inverse = small.tile([P, TILES], F32, tag="inverse")
+            nc.vector.reciprocal(out=inverse[:], in_=total[:])
+            ctx = work.tile([P, TILES, D], F32, tag="ctx")
+            nc.vector.tensor_tensor(
+                out=ctx[:], in0=ctx_acc[head][:], in1=inverse[:].unsqueeze(2).to_broadcast([P, TILES, D]), op=ALU.mult
+            )
+            nc.sync.dma_start(out=out_0[b, :, h * D : (h + 1) * D].rearrange("(i p) d -> p i d", p=P), in_=ctx[:])
+
+        def in_range(n):
+            return 0 <= n < STEPS
+
+        stack.enter_context(tc.manual_schedule())
+        for j in range(-VALUES_AHEAD, STEPS + FINISH_BEHIND):
+            if in_range(j - FINISH_BEHIND) and (j - FINISH_BEHIND) % TILES == TILES - 1:
+                finish_head((j - FINISH_BEHIND) // TILES)
+            if in_range(j) and j % STEPS_PER_BATCH == 0 and j // STEPS_PER_BATCH + 2 < B:
+                load_batch(j // STEPS_PER_BATCH + 2)
+            if in_range(j):
+                exponentials(j)
+            if in_range(j - TRANSPOSE_BEHIND):
+                transpose_e(j - TRANSPOSE_BEHIND)
+            if in_range(j + PREPARE_AHEAD):
+                prepare_transposes(j + PREPARE_AHEAD)
+            if in_range(j - ATTEND_BEHIND):
+                attend(j - ATTEND_BEHIND)
+            if in_range(j + SCORES_AHEAD):
+                scores(j + SCORES_AHEAD)
+            if in_range(j + MAX_AHEAD):
+                row_max(j + MAX_AHEAD)
+            if in_range(j - QUANTISE_BEHIND):
+                quantise_e(j - QUANTISE_BEHIND)
+            if in_range(j - TRANSPOSE_BEHIND):
+                copy_e(j - TRANSPOSE_BEHIND)
+            if in_range(j + PREPARE_AHEAD):
+                prepare_copy(j + PREPARE_AHEAD)
+            b_next, step = divmod(j + VALUES_AHEAD, STEPS_PER_BATCH)
+            if b_next < B:
+                prepare_values(b_next, step)

@@ -33,7 +33,6 @@ QUANTISE_BEHIND = 2
 ATTEND_BEHIND = 3
 FINISH_BEHIND = 4
 VALUES_AHEAD = 10
-VECTOR_COPY_PERIOD = 3
 
 
 def tile_attentionlayer_pa_t_kernel(tc, q, k_cache, k_new, x, Wv, bv, v_cache, out_0, out_1):
@@ -44,6 +43,7 @@ def tile_attentionlayer_pa_t_kernel(tc, q, k_cache, k_new, x, Wv, bv, v_cache, o
         heads = stack.enter_context(tc.tile_pool(name="heads", bufs=3))
         small = stack.enter_context(tc.tile_pool(name="small", bufs=6))
         work = stack.enter_context(tc.tile_pool(name="work", bufs=3))
+        codes = stack.enter_context(tc.tile_pool(name="codes", bufs=2 * TILES))
         values = stack.enter_context(tc.tile_pool(name="values", bufs=2))
         psum_scores = stack.enter_context(tc.psum_pool(name="psum_scores", bufs=4))
         psum_turn = stack.enter_context(tc.psum_pool(name="psum_turn", bufs=3))
@@ -199,16 +199,20 @@ def tile_attentionlayer_pa_t_kernel(tc, q, k_cache, k_new, x, Wv, bv, v_cache, o
                 dT[head] = qkT
             nc.scalar.copy(out=dT[head][:, :, r * P : (r + 1) * P], in_=turned[n][:])
 
-        def scores(n):
+        def scores_cache(n):
+            head, i = divmod(n, TILES)
+            cache = psum_scores.tile([P, T], F32, tag="scores")
+            nc.tensor.matmul(out=cache[:], lhsT=dT[head][:, 0, i * P : (i + 1) * P], rhs=dT[head][:, 1, :], start=True, stop=True)
+            score_banks[n] = [cache[:]]
+
+        def scores_new(n):
             head, i = divmod(n, TILES)
             qT = dT[head][:, 0, i * P : (i + 1) * P]
             seen = (i + 1) * P
-            cache = psum_scores.tile([P, T], F32, tag="scores")
-            nc.tensor.matmul(out=cache[:], lhsT=qT, rhs=dT[head][:, 1, :], start=True, stop=True)
             new = psum_scores.tile([P, S], F32, tag="scores")
             nc.tensor.matmul(out=new[:, :seen], lhsT=qT, rhs=dT[head][:, 2, :seen], start=True, stop=False)
             nc.tensor.matmul(out=new[:, i * P : seen], lhsT=ident_bf[:], rhs=mask_bf[:], start=False, stop=True)
-            score_banks[n] = [cache[:], new[:, :seen]]
+            score_banks[n].append(new[:, :seen])
 
         def row_max(n):
             both = small.tile([P, 2], F32, tag="both")
@@ -242,34 +246,33 @@ def tile_attentionlayer_pa_t_kernel(tc, q, k_cache, k_new, x, Wv, bv, v_cache, o
 
         def copy_e(n):
             eg = work.tile([P, 2 * P * PACK], BF16, tag="eg", align_bytes=64)
-            copy = nc.vector.tensor_copy if n % VECTOR_COPY_PERIOD == 0 else nc.scalar.copy
-            copy(
+            nc.scalar.copy(
                 out=eg[:].bitcast(F32).rearrange("p (g c u) -> p g c u", g=2, u=2),
                 in_=e_turned[n][:].rearrange("p (g u) c -> p g c u", g=2),
             )
             e_grouped[n] = eg
 
         def quantise_e(n):
-            ec = work.tile([P, 2 * P], U32, tag="ec", align_bytes=64)
-            es = work.tile([P, 2 * P], U8, tag="es", align_bytes=64)
+            ec = codes.tile([P, 2 * P], U32, tag="ec", align_bytes=64)
+            es = codes.tile([P, 2 * P], U8, tag="es", align_bytes=64)
             nc.vector.quantize_mx(out=ec[:].bitcast(FP8X4), scales=es[:], in_=e_grouped[n][:])
             e_codes[n], e_scales[n] = ec, es
 
-        def attend(n):
-            head, i = divmod(n, TILES)
+        def attend(head):
             b, h = divmod(head, H)
-            if i == 0:
-                acc = psum_ctx.tile([P, TILES, D], F32, tag="ctx")
-                ctx_acc[head] = acc
-            for g in range(2):
-                nc.tensor.matmul_mx(
-                    out=ctx_acc[head][:, i, :],
-                    lhsT=e_codes[n][:, g * P : (g + 1) * P].bitcast(FP8X4),
-                    lhsT_scale=e_scales[n][:, g * P : (g + 1) * P],
-                    rhs=v_codes[b][g][:, h * D : (h + 1) * D].bitcast(FP8X4),
-                    rhs_scale=v_scales[b][g][:, h * D : (h + 1) * D],
-                    start=(g == 0), stop=(g == 1),
-                )
+            acc = psum_ctx.tile([P, TILES, D], F32, tag="ctx")
+            for i in range(TILES):
+                n = head * TILES + i
+                for g in range(2):
+                    nc.tensor.matmul_mx(
+                        out=acc[:, i, :],
+                        lhsT=e_codes[n][:, g * P : (g + 1) * P].bitcast(FP8X4),
+                        lhsT_scale=e_scales[n][:, g * P : (g + 1) * P],
+                        rhs=v_codes[b][g][:, h * D : (h + 1) * D].bitcast(FP8X4),
+                        rhs_scale=v_scales[b][g][:, h * D : (h + 1) * D],
+                        start=(g == 0), stop=(g == 1),
+                    )
+            ctx_acc[head] = acc
 
         def finish_head(head):
             b, h = divmod(head, H)
@@ -296,12 +299,14 @@ def tile_attentionlayer_pa_t_kernel(tc, q, k_cache, k_new, x, Wv, bv, v_cache, o
                 exponentials(j)
             if in_range(j - TRANSPOSE_BEHIND):
                 transpose_e(j - TRANSPOSE_BEHIND)
+            if in_range(j - ATTEND_BEHIND) and (j - ATTEND_BEHIND) % TILES == TILES - 1:
+                attend((j - ATTEND_BEHIND) // TILES)
+            if in_range(j + SCORES_AHEAD):
+                scores_cache(j + SCORES_AHEAD)
             if in_range(j + PREPARE_AHEAD):
                 prepare_transposes(j + PREPARE_AHEAD)
-            if in_range(j - ATTEND_BEHIND):
-                attend(j - ATTEND_BEHIND)
             if in_range(j + SCORES_AHEAD):
-                scores(j + SCORES_AHEAD)
+                scores_new(j + SCORES_AHEAD)
             if in_range(j + MAX_AHEAD):
                 row_max(j + MAX_AHEAD)
             if in_range(j - QUANTISE_BEHIND):

@@ -210,7 +210,7 @@ def tile_attentionlayer_pa_t_kernel(tc, q, k_cache, k_new, x, Wv, bv, v_cache, o
             qT = dT[head][:, 0, i * P : (i + 1) * P]
             seen = (i + 1) * P
             new = psum_scores.tile([P, S], F32, tag="scores")
-            nc.tensor.matmul(out=new[:, :seen], lhsT=qT, rhs=dT[head][:, 2, :seen], start=True, stop=False)
+            nc.tensor.matmul(out=new[:], lhsT=qT, rhs=dT[head][:, 2, :], start=True, stop=False)
             nc.tensor.matmul(out=new[:, i * P : seen], lhsT=ident_bf[:], rhs=mask_bf[:], start=False, stop=True)
             score_banks[n].append(new[:, :seen])
 

@@ -289,7 +289,6 @@ def tile_attentionlayer_pa_t_kernel(tc, q, k_cache, k_new, x, Wv, bv, v_cache, o
         def in_range(n):
             return 0 <= n < STEPS
 
-        stack.enter_context(tc.manual_schedule())
         for j in range(-VALUES_AHEAD, STEPS + FINISH_BEHIND):
             if in_range(j - FINISH_BEHIND) and (j - FINISH_BEHIND) % TILES == TILES - 1:
                 finish_head((j - FINISH_BEHIND) // TILES)

@@ -32,7 +32,8 @@ TRANSPOSE_BEHIND = 1
 QUANTISE_BEHIND = 2
 ATTEND_BEHIND = 3
 FINISH_BEHIND = 4
-VALUES_AHEAD = 10
+HEADS_LOADED_AHEAD = 4
+VALUES_AHEAD = 6
 
 
 def tile_attentionlayer_pa_t_kernel(tc, q, k_cache, k_new, x, Wv, bv, v_cache, out_0, out_1):
@@ -51,25 +52,32 @@ def tile_attentionlayer_pa_t_kernel(tc, q, k_cache, k_new, x, Wv, bv, v_cache, o
 
         q_sb, kc_sb, kn_sb, x_sb, vc_sb = {}, {}, {}, {}, {}
 
-        def load_batch(b):
+        def load_head(head):
+            b, h = divmod(head, H)
+            q_t = loads.tile([P, TILES, D], BF16, tag="q", bufs=HEADS_LOADED_AHEAD + 2)
+            nc.sync.dma_start(out=q_t[:], in_=q[b, h].rearrange("(i p) d -> p i d", p=P))
+            kc_t = loads.tile([P, TILES, D], BF16, tag="kc", bufs=HEADS_LOADED_AHEAD + 2)
+            nc.sync.dma_start(out=kc_t[:], in_=k_cache[b, h].rearrange("(t p) d -> p t d", p=P))
+            kn_t = loads.tile([P, TILES, D], BF16, tag="kn", bufs=HEADS_LOADED_AHEAD + 2)
+            nc.sync.dma_start(out=kn_t[:], in_=k_new[b, h].rearrange("(t p) d -> p t d", p=P))
+            q_sb[head], kc_sb[head], kn_sb[head] = q_t, kc_t, kn_t
+
+        def load_values(b):
             x_t = loads.tile([P, TILES, DIM], BF16, tag="x")
             nc.sync.dma_start(out=x_t[:].rearrange("p (u e) f -> p u (e f)", e=2), in_=x[b].rearrange("(u p e) f -> p u (e f)", p=P, e=2))
-            q_t = loads.tile([P, H * TILES, D], BF16, tag="q")
-            nc.sync.dma_start(out=q_t[:], in_=q[b].rearrange("h (i p) d -> p (h i) d", p=P))
-            kc_t = loads.tile([P, H * TILES, D], BF16, tag="kc")
-            nc.sync.dma_start(out=kc_t[:], in_=k_cache[b].rearrange("h (t p) d -> p (h t) d", p=P))
-            kn_t = loads.tile([P, H * TILES, D], BF16, tag="kn")
-            nc.sync.dma_start(out=kn_t[:], in_=k_new[b].rearrange("h (t p) d -> p (h t) d", p=P))
             vc_t = loads.tile([P, H, PACK * D], BF16, tag="vc")
             nc.sync.dma_start(out=vc_t[:].rearrange("p h (u r) -> p (h u) r", u=2), in_=v_cache[b].rearrange("h (u p e) d -> p (h u) (e d)", p=P, e=2))
-            x_sb[b], q_sb[b], kc_sb[b], kn_sb[b], vc_sb[b] = x_t, q_t, kc_t, kn_t, vc_t
+            x_sb[b], vc_sb[b] = x_t, vc_t
 
+        load_head(0)
         w_sb = const.tile([P, TILES, DIM], BF16)
         nc.sync.dma_start(out=w_sb[:], in_=Wv.rearrange("(r p) k -> p r k", p=P))
-        load_batch(0)
+        load_values(0)
         bias_bf = const.tile([P, DIM], BF16)
         nc.sync.dma_start(out=bias_bf[:], in_=bv.partition_broadcast(P))
-        load_batch(1)
+        for head in range(1, HEADS_LOADED_AHEAD):
+            load_head(head)
+        load_values(1)
 
         ident_bf = const.tile([P, P], BF16)
         make_identity(nc, ident_bf[:])
@@ -185,11 +193,10 @@ def tile_attentionlayer_pa_t_kernel(tc, q, k_cache, k_new, x, Wv, bv, v_cache, o
 
         def prepare_transposes(n):
             head, r = divmod(n, TILES)
-            b, h = divmod(head, H)
             blocks = psum_turn.tile([P, 3, P], BF16, tag="turn")
-            nc.tensor.transpose(out=blocks[:, 0, :], in_=q_sb[b][:, h * TILES + r, :], identity=ident_bf[:])
-            nc.tensor.transpose(out=blocks[:, 1, :], in_=kc_sb[b][:, h * TILES + r, :], identity=ident_bf[:])
-            nc.tensor.transpose(out=blocks[:, 2, :], in_=kn_sb[b][:, h * TILES + r, :], identity=ident_bf[:])
+            nc.tensor.transpose(out=blocks[:, 0, :], in_=q_sb[head][:, r, :], identity=ident_bf[:])
+            nc.tensor.transpose(out=blocks[:, 1, :], in_=kc_sb[head][:, r, :], identity=ident_bf[:])
+            nc.tensor.transpose(out=blocks[:, 2, :], in_=kn_sb[head][:, r, :], identity=ident_bf[:])
             turned[n] = blocks
 
         def prepare_copy(n):
@@ -197,7 +204,7 @@ def tile_attentionlayer_pa_t_kernel(tc, q, k_cache, k_new, x, Wv, bv, v_cache, o
             if r == 0:
                 qkT = heads.tile([P, 3, S], BF16, tag="qkT")
                 dT[head] = qkT
-            nc.scalar.copy(out=dT[head][:, :, r * P : (r + 1) * P], in_=turned[n][:])
+            nc.vector.tensor_copy(out=dT[head][:, :, r * P : (r + 1) * P], in_=turned[n][:])
 
         def scores_cache(n):
             head, i = divmod(n, TILES)
@@ -219,7 +226,7 @@ def tile_attentionlayer_pa_t_kernel(tc, q, k_cache, k_new, x, Wv, bv, v_cache, o
             for g in range(2):
                 nc.vector.tensor_reduce(out=both[:, g : g + 1], in_=score_banks[n][g], axis=AXIS.X, op=ALU.max)
             nm = small.tile([P, 1], F32, tag="nm")
-            nc.vector.tensor_scalar(
+            nc.gpsimd.tensor_scalar(
                 out=nm[:], in0=both[:, 0:1], scalar1=both[:, 1:2], scalar2=-SCALE, op0=ALU.max, op1=ALU.mult
             )
             neg_max[n] = nm
@@ -293,7 +300,9 @@ def tile_attentionlayer_pa_t_kernel(tc, q, k_cache, k_new, x, Wv, bv, v_cache, o
             if in_range(j - FINISH_BEHIND) and (j - FINISH_BEHIND) % TILES == TILES - 1:
                 finish_head((j - FINISH_BEHIND) // TILES)
             if in_range(j) and j % STEPS_PER_BATCH == 0 and j // STEPS_PER_BATCH + 2 < B:
-                load_batch(j // STEPS_PER_BATCH + 2)
+                load_values(j // STEPS_PER_BATCH + 2)
+            if in_range(j + HEADS_LOADED_AHEAD * TILES) and j >= 0 and j % TILES == 0:
+                load_head(j // TILES + HEADS_LOADED_AHEAD)
             if in_range(j):
                 exponentials(j)
             if in_range(j - TRANSPOSE_BEHIND):

@@ -11,7 +11,6 @@ U8 = mybir.dt.uint8
 FP8X4 = mybir.dt.float8_e4m3fn_x4
 ALU = mybir.AluOpType
 ACT = mybir.ActivationFunctionType
-AXIS = mybir.AxisListType
 
 P = 128
 PACK = 4
@@ -25,15 +24,15 @@ MASKED = -1.0e30
 
 FLOPS = 2 * B * H * S * (T + S) * D * 2 + 2 * B * S * DIM * DIM
 
-PREPARE_AHEAD = 6
-SCORES_AHEAD = 2
-MAX_AHEAD = 1
+PREPARE_AHEAD = 7
+SCORES_AHEAD = 3
+MAX_AHEAD = 2
 TRANSPOSE_BEHIND = 1
 QUANTISE_BEHIND = 2
 ATTEND_BEHIND = 3
 FINISH_BEHIND = 4
 HEADS_LOADED_AHEAD = 4
-VALUES_AHEAD = 6
+VALUES_AHEAD = 7
 
 
 def tile_attentionlayer_pa_t_kernel(tc, q, k_cache, k_new, x, Wv, bv, v_cache, out_0, out_1):
@@ -187,8 +186,8 @@ def tile_attentionlayer_pa_t_kernel(tc, q, k_cache, k_new, x, Wv, bv, v_cache, o
             elif step == 4 + TILES:
                 quantise_v(b)
 
-        turned, dT, score_banks, neg_max, row_sums, e_turned, e_grouped, e_codes, e_scales, ctx_acc = (
-            {}, {}, {}, {}, {}, {}, {}, {}, {}, {},
+        turned, dT, score_banks, neg_scores, neg_max, row_sums, e_turned, e_grouped, e_codes, e_scales, ctx_acc = (
+            {}, {}, {}, {}, {}, {}, {}, {}, {}, {}, {},
         )
 
         def prepare_transposes(n):
@@ -204,7 +203,8 @@ def tile_attentionlayer_pa_t_kernel(tc, q, k_cache, k_new, x, Wv, bv, v_cache, o
             if r == 0:
                 qkT = heads.tile([P, 3, S], BF16, tag="qkT")
                 dT[head] = qkT
-            nc.vector.tensor_copy(out=dT[head][:, :, r * P : (r + 1) * P], in_=turned[n][:])
+            copy = nc.scalar.copy if n % 2 == 0 else nc.vector.tensor_copy
+            copy(out=dT[head][:, :, r * P : (r + 1) * P], in_=turned[n][:])
 
         def scores_cache(n):
             head, i = divmod(n, TILES)
@@ -222,26 +222,31 @@ def tile_attentionlayer_pa_t_kernel(tc, q, k_cache, k_new, x, Wv, bv, v_cache, o
             score_banks[n].append(new[:, :seen])
 
         def row_max(n):
-            both = small.tile([P, 2], F32, tag="both")
-            for g in range(2):
-                nc.vector.tensor_reduce(out=both[:, g : g + 1], in_=score_banks[n][g], axis=AXIS.X, op=ALU.max)
-            nm = small.tile([P, 1], F32, tag="nm")
-            nc.gpsimd.tensor_scalar(
-                out=nm[:], in0=both[:, 0:1], scalar1=both[:, 1:2], scalar2=-SCALE, op0=ALU.max, op1=ALU.mult
+            i = n % TILES
+            seen = (i + 1) * P
+            neg_s = work.tile([P, T + S], F32, tag="neg_s", bufs=4)
+            first = small.tile([P, 1], F32, tag="first")
+            nc.vector.tensor_scalar(
+                out=neg_s[:, :T], in0=score_banks[n][0], scalar1=-SCALE, scalar2=None,
+                op0=ALU.mult, op1=ALU.min, accum_out=first[:],
             )
-            neg_max[n] = nm
+            nm = small.tile([P, 1], F32, tag="nm")
+            nc.vector.tensor_scalar(
+                out=neg_s[:, T : T + seen], in0=score_banks[n][1], scalar1=-SCALE, scalar2=first[:],
+                op0=ALU.mult, op1=ALU.min, accum_out=nm[:],
+            )
+            neg_scores[n], neg_max[n] = neg_s, nm
 
         def exponentials(n):
             head, i = divmod(n, TILES)
             if i == 0:
-                sums = small.tile([P, TILES, 2], F32, tag="sums")
+                sums = small.tile([P, TILES], F32, tag="sums")
                 row_sums[head] = sums
-            seen = (i + 1) * P
-            for g, cols in enumerate([slice(0, T), slice(T, T + seen)]):
-                nc.scalar.activation(
-                    out=e_sb[i][:, cols], in_=score_banks[n][g], func=ACT.Exp,
-                    bias=neg_max[n][:], scale=SCALE, accum_out=row_sums[head][:, i, g : g + 1],
-                )
+            keys = T + (i + 1) * P
+            nc.scalar.activation(
+                out=e_sb[i][:, :keys], in_=neg_scores[n][:, :keys], func=ACT.Exp,
+                bias=neg_max[n][:], scale=-1.0, accum_out=row_sums[head][:, i : i + 1],
+            )
 
         def transpose_e(n):
             i = n % TILES
@@ -283,10 +288,8 @@ def tile_attentionlayer_pa_t_kernel(tc, q, k_cache, k_new, x, Wv, bv, v_cache, o
 
         def finish_head(head):
             b, h = divmod(head, H)
-            total = small.tile([P, TILES], F32, tag="total")
-            nc.vector.tensor_reduce(out=total[:], in_=row_sums[head][:], axis=AXIS.X, op=ALU.add)
             inverse = small.tile([P, TILES], F32, tag="inverse")
-            nc.vector.reciprocal(out=inverse[:], in_=total[:])
+            nc.vector.reciprocal(out=inverse[:], in_=row_sums[head][:])
             ctx = work.tile([P, TILES, D], F32, tag="ctx")
             nc.vector.tensor_tensor(
                 out=ctx[:], in0=ctx_acc[head][:], in1=inverse[:].unsqueeze(2).to_broadcast([P, TILES, D]), op=ALU.mult

@@ -121,9 +121,9 @@ def tile_attentionlayer_pa_t_kernel(tc, q, k_cache, k_new, x, Wv, bv, v_cache, o
 
         x_grouped, x_codes, x_scales, v_new, v_grouped, v_codes, v_scales = {}, {}, {}, {}, {}, {}, {}
 
-        def regroup(grouped, rows):
+        def regroup(grouped, rows, h):
             nc.gpsimd.tensor_scalar(
-                out=grouped[:].rearrange("p (h d t) -> p h d t", h=H, t=PACK),
+                out=grouped[:, h * D * PACK : (h + 1) * D * PACK].rearrange("p (d t) -> p d t", t=PACK),
                 in0=rows, scalar1=1.0, scalar2=0.0, op0=ALU.mult, op1=ALU.add,
             )
 
@@ -131,9 +131,12 @@ def tile_attentionlayer_pa_t_kernel(tc, q, k_cache, k_new, x, Wv, bv, v_cache, o
             xg = values.tile([P, S * PACK], BF16, tag="xg", align_bytes=64)
             turn_words(x_sb[b], xg)
             x_grouped[b] = xg
-            vg_cache = values.tile([P, DIM * PACK], BF16, tag="vg_cache", align_bytes=64)
-            regroup(vg_cache, vc_sb[b][:].rearrange("p h (t d) -> p h d t", t=PACK))
-            v_grouped[b] = [vg_cache]
+
+        def regroup_v_cache(b, h):
+            if h == 0:
+                vg_cache = values.tile([P, DIM * PACK], BF16, tag="vg_cache", align_bytes=64)
+                v_grouped[b] = [vg_cache]
+            regroup(v_grouped[b][0], vc_sb[b][:, h, :].rearrange("p (t d) -> p d t", t=PACK), h)
 
         def quantise_x(b):
             xc = values.tile([P, S], U32, tag="xc", align_bytes=64)
@@ -159,11 +162,12 @@ def tile_attentionlayer_pa_t_kernel(tc, q, k_cache, k_new, x, Wv, bv, v_cache, o
                 op=ALU.add,
             )
 
-        def regroup_v_new(b):
-            nc.sync.dma_start(out=out_1[b].rearrange("h (u p e) d -> p (h u) (e d)", p=P, e=2), in_=v_new[b][:].rearrange("p h (u e) d -> p (h u) (e d)", e=2))
-            vg_new = values.tile([P, DIM * PACK], BF16, tag="vg_new", align_bytes=64)
-            regroup(vg_new, v_new[b][:].rearrange("p h t d -> p h d t"))
-            v_grouped[b].append(vg_new)
+        def regroup_v_new(b, h):
+            if h == 0:
+                nc.sync.dma_start(out=out_1[b].rearrange("h (u p e) d -> p (h u) (e d)", p=P, e=2), in_=v_new[b][:].rearrange("p h (u e) d -> p (h u) (e d)", e=2))
+                vg_new = values.tile([P, DIM * PACK], BF16, tag="vg_new", align_bytes=64)
+                v_grouped[b].append(vg_new)
+            regroup(v_grouped[b][1], v_new[b][:, h, :, :].rearrange("p t d -> p d t"), h)
 
         def quantise_v(b):
             v_codes[b], v_scales[b] = [], []
@@ -181,10 +185,12 @@ def tile_attentionlayer_pa_t_kernel(tc, q, k_cache, k_new, x, Wv, bv, v_cache, o
                 quantise_x(b)
             elif step < 2 + TILES:
                 project(b, step - 2)
-            elif step == 2 + TILES:
-                regroup_v_new(b)
-            elif step == 4 + TILES:
+            elif step == 7 + TILES:
                 quantise_v(b)
+            if 1 <= step < 1 + H:
+                regroup_v_cache(b, step - 1)
+            elif 2 + TILES <= step < 2 + TILES + H:
+                regroup_v_new(b, step - 2 - TILES)
 
         turned, dT, score_banks, neg_scores, neg_max, row_sums, e_turned, e_grouped, e_codes, e_scales, ctx_acc = (
             {}, {}, {}, {}, {}, {}, {}, {}, {}, {}, {},

@@ -192,25 +192,25 @@ def tile_attentionlayer_pa_t_kernel(tc, q, k_cache, k_new, x, Wv, bv, v_cache, o
             elif 2 + TILES <= step < 2 + TILES + H:
                 regroup_v_new(b, step - 2 - TILES)
 
-        turned, dT, score_banks, neg_scores, neg_max, row_sums, e_turned, e_grouped, e_codes, e_scales, ctx_acc = (
-            {}, {}, {}, {}, {}, {}, {}, {}, {}, {}, {},
-        )
+        turned, dT, score_banks, neg_scores, first_min, neg_max, row_sums, inverses = {}, {}, {}, {}, {}, {}, {}, {}
+        e_turned, e_grouped, e_codes, e_scales, ctx_acc = {}, {}, {}, {}, {}
 
         def prepare_transposes(n):
             head, r = divmod(n, TILES)
-            blocks = psum_turn.tile([P, 3, P], BF16, tag="turn")
-            nc.tensor.transpose(out=blocks[:, 0, :], in_=q_sb[head][:, r, :], identity=ident_bf[:])
-            nc.tensor.transpose(out=blocks[:, 1, :], in_=kc_sb[head][:, r, :], identity=ident_bf[:])
-            nc.tensor.transpose(out=blocks[:, 2, :], in_=kn_sb[head][:, r, :], identity=ident_bf[:])
-            turned[n] = blocks
+            if r < 3:
+                rows = (q_sb, kc_sb, kn_sb)[r][head]
+                blocks = psum_turn.tile([P, TILES, P], BF16, tag="turn")
+                for t in range(TILES):
+                    nc.tensor.transpose(out=blocks[:, t, :], in_=rows[:, t, :], identity=ident_bf[:])
+                turned[n] = blocks
 
         def prepare_copy(n):
             head, r = divmod(n, TILES)
             if r == 0:
                 qkT = heads.tile([P, 3, S], BF16, tag="qkT")
                 dT[head] = qkT
-            copy = nc.scalar.copy if n % 2 == 0 else nc.vector.tensor_copy
-            copy(out=dT[head][:, :, r * P : (r + 1) * P], in_=turned[n][:])
+            if r < 3:
+                nc.scalar.copy(out=dT[head][:, r, :], in_=turned[n][:].rearrange("p t c -> p (t c)"))
 
         def scores_cache(n):
             head, i = divmod(n, TILES)
@@ -227,21 +227,23 @@ def tile_attentionlayer_pa_t_kernel(tc, q, k_cache, k_new, x, Wv, bv, v_cache, o
             nc.tensor.matmul(out=new[:, i * P : seen], lhsT=ident_bf[:], rhs=mask_bf[:], start=False, stop=True)
             score_banks[n].append(new[:, :seen])
 
-        def row_max(n):
-            i = n % TILES
-            seen = (i + 1) * P
+        def row_max_cache(n):
             neg_s = work.tile([P, T + S], F32, tag="neg_s", bufs=4)
             first = small.tile([P, 1], F32, tag="first")
             nc.vector.tensor_scalar(
                 out=neg_s[:, :T], in0=score_banks[n][0], scalar1=-SCALE, scalar2=None,
                 op0=ALU.mult, op1=ALU.min, accum_out=first[:],
             )
+            neg_scores[n], first_min[n] = neg_s, first
+
+        def row_max_new(n):
+            seen = (n % TILES + 1) * P
             nm = small.tile([P, 1], F32, tag="nm")
             nc.vector.tensor_scalar(
-                out=neg_s[:, T : T + seen], in0=score_banks[n][1], scalar1=-SCALE, scalar2=first[:],
+                out=neg_scores[n][:, T : T + seen], in0=score_banks[n][1], scalar1=-SCALE, scalar2=first_min[n][:],
                 op0=ALU.mult, op1=ALU.min, accum_out=nm[:],
             )
-            neg_scores[n], neg_max[n] = neg_s, nm
+            neg_max[n] = nm
 
         def exponentials(n):
             head, i = divmod(n, TILES)
@@ -292,13 +294,16 @@ def tile_attentionlayer_pa_t_kernel(tc, q, k_cache, k_new, x, Wv, bv, v_cache, o
                     )
             ctx_acc[head] = acc
 
-        def finish_head(head):
-            b, h = divmod(head, H)
+        def invert_sums(head):
             inverse = small.tile([P, TILES], F32, tag="inverse")
             nc.vector.reciprocal(out=inverse[:], in_=row_sums[head][:])
+            inverses[head] = inverse
+
+        def finish_head(head):
+            b, h = divmod(head, H)
             ctx = work.tile([P, TILES, D], F32, tag="ctx")
             nc.vector.tensor_tensor(
-                out=ctx[:], in0=ctx_acc[head][:], in1=inverse[:].unsqueeze(2).to_broadcast([P, TILES, D]), op=ALU.mult
+                out=ctx[:], in0=ctx_acc[head][:], in1=inverses[head][:].unsqueeze(2).to_broadcast([P, TILES, D]), op=ALU.mult
             )
             nc.sync.dma_start(out=out_0[b, :, h * D : (h + 1) * D].rearrange("(i p) d -> p i d", p=P), in_=ctx[:])
 
@@ -317,6 +322,7 @@ def tile_attentionlayer_pa_t_kernel(tc, q, k_cache, k_new, x, Wv, bv, v_cache, o
             if in_range(j - TRANSPOSE_BEHIND):
                 transpose_e(j - TRANSPOSE_BEHIND)
             if in_range(j - ATTEND_BEHIND) and (j - ATTEND_BEHIND) % TILES == TILES - 1:
+                invert_sums((j - ATTEND_BEHIND) // TILES)
                 attend((j - ATTEND_BEHIND) // TILES)
             if in_range(j + SCORES_AHEAD):
                 scores_cache(j + SCORES_AHEAD)
@@ -325,7 +331,9 @@ def tile_attentionlayer_pa_t_kernel(tc, q, k_cache, k_new, x, Wv, bv, v_cache, o
             if in_range(j + SCORES_AHEAD):
                 scores_new(j + SCORES_AHEAD)
             if in_range(j + MAX_AHEAD):
-                row_max(j + MAX_AHEAD)
+                row_max_new(j + MAX_AHEAD)
+            if in_range(j + MAX_AHEAD + 1):
+                row_max_cache(j + MAX_AHEAD + 1)
             if in_range(j - QUANTISE_BEHIND):
                 quantise_e(j - QUANTISE_BEHIND)
             if in_range(j - TRANSPOSE_BEHIND):

@@ -310,9 +310,8 @@ def tile_attentionlayer_pa_t_kernel(tc, q, k_cache, k_new, x, Wv, bv, v_cache, o
         def in_range(n):
             return 0 <= n < STEPS
 
+        stack.enter_context(tc.manual_schedule())
         for j in range(-VALUES_AHEAD, STEPS + FINISH_BEHIND):
-            if in_range(j - FINISH_BEHIND) and (j - FINISH_BEHIND) % TILES == TILES - 1:
-                finish_head((j - FINISH_BEHIND) // TILES)
             if in_range(j) and j % STEPS_PER_BATCH == 0 and j // STEPS_PER_BATCH + 2 < B:
                 load_values(j // STEPS_PER_BATCH + 2)
             if in_range(j + HEADS_LOADED_AHEAD * TILES) and j >= 0 and j % TILES == 0:
@@ -321,9 +320,8 @@ def tile_attentionlayer_pa_t_kernel(tc, q, k_cache, k_new, x, Wv, bv, v_cache, o
                 exponentials(j)
             if in_range(j - TRANSPOSE_BEHIND):
                 transpose_e(j - TRANSPOSE_BEHIND)
-            if in_range(j - ATTEND_BEHIND) and (j - ATTEND_BEHIND) % TILES == TILES - 1:
-                invert_sums((j - ATTEND_BEHIND) // TILES)
-                attend((j - ATTEND_BEHIND) // TILES)
+            if in_range(j - QUANTISE_BEHIND):
+                quantise_e(j - QUANTISE_BEHIND)
             if in_range(j + SCORES_AHEAD):
                 scores_cache(j + SCORES_AHEAD)
             if in_range(j + PREPARE_AHEAD):
@@ -332,10 +330,13 @@ def tile_attentionlayer_pa_t_kernel(tc, q, k_cache, k_new, x, Wv, bv, v_cache, o
                 scores_new(j + SCORES_AHEAD)
             if in_range(j + MAX_AHEAD):
                 row_max_new(j + MAX_AHEAD)
+            if in_range(j - FINISH_BEHIND) and (j - FINISH_BEHIND) % TILES == TILES - 1:
+                finish_head((j - FINISH_BEHIND) // TILES)
             if in_range(j + MAX_AHEAD + 1):
                 row_max_cache(j + MAX_AHEAD + 1)
-            if in_range(j - QUANTISE_BEHIND):
-                quantise_e(j - QUANTISE_BEHIND)
+            if in_range(j - ATTEND_BEHIND) and (j - ATTEND_BEHIND) % TILES == TILES - 1:
+                invert_sums((j - ATTEND_BEHIND) // TILES)
+                attend((j - ATTEND_BEHIND) // TILES)
             if in_range(j - TRANSPOSE_BEHIND):
                 copy_e(j - TRANSPOSE_BEHIND)
             if in_range(j + PREPARE_AHEAD):

@@ -33,6 +33,7 @@ ATTEND_BEHIND = 3
 FINISH_BEHIND = 4
 HEADS_LOADED_AHEAD = 4
 VALUES_AHEAD = 7
+FIRST_VALUES_AHEAD = 3
 
 
 def tile_attentionlayer_pa_t_kernel(tc, q, k_cache, k_new, x, Wv, bv, v_cache, out_0, out_1):
@@ -61,22 +62,28 @@ def tile_attentionlayer_pa_t_kernel(tc, q, k_cache, k_new, x, Wv, bv, v_cache, o
             nc.sync.dma_start(out=kn_t[:], in_=k_new[b, h].rearrange("(t p) d -> p t d", p=P))
             q_sb[head], kc_sb[head], kn_sb[head] = q_t, kc_t, kn_t
 
-        def load_values(b):
+        def load_x(b):
             x_t = loads.tile([P, TILES, DIM], BF16, tag="x")
             nc.sync.dma_start(out=x_t[:].rearrange("p (u e) f -> p u (e f)", e=2), in_=x[b].rearrange("(u p e) f -> p u (e f)", p=P, e=2))
+            x_sb[b] = x_t
+
+        def load_v_cache(b):
             vc_t = loads.tile([P, H, PACK * D], BF16, tag="vc")
             nc.sync.dma_start(out=vc_t[:].rearrange("p h (u r) -> p (h u) r", u=2), in_=v_cache[b].rearrange("h (u p e) d -> p (h u) (e d)", p=P, e=2))
-            x_sb[b], vc_sb[b] = x_t, vc_t
+            vc_sb[b] = vc_t
 
         load_head(0)
         w_sb = const.tile([P, TILES, DIM], BF16)
         nc.sync.dma_start(out=w_sb[:], in_=Wv.rearrange("(r p) k -> p r k", p=P))
-        load_values(0)
+        load_x(0)
+        load_head(1)
         bias_bf = const.tile([P, DIM], BF16)
         nc.sync.dma_start(out=bias_bf[:], in_=bv.partition_broadcast(P))
-        for head in range(1, HEADS_LOADED_AHEAD):
+        load_v_cache(0)
+        for head in range(2, HEADS_LOADED_AHEAD):
             load_head(head)
-        load_values(1)
+        load_x(1)
+        load_v_cache(1)
 
         ident_bf = const.tile([P, P], BF16)
         make_identity(nc, ident_bf[:])
@@ -91,7 +98,7 @@ def tile_attentionlayer_pa_t_kernel(tc, q, k_cache, k_new, x, Wv, bv, v_cache, o
         mask_bf = const.tile([P, P], BF16)
         nc.vector.tensor_copy(out=mask_bf[:], in_=mask_f32[:])
         bias = const.tile([P, DIM], F32)
-        nc.vector.tensor_copy(out=bias[:], in_=bias_bf[:])
+        nc.gpsimd.tensor_scalar(out=bias[:], in0=bias_bf[:], scalar1=1.0, scalar2=0.0, op0=ALU.mult, op1=ALU.add)
         e_sb = []
         for i in range(TILES):
             e_t = const.tile([P, T + S], BF16, name="e%d" % i)
@@ -99,7 +106,7 @@ def tile_attentionlayer_pa_t_kernel(tc, q, k_cache, k_new, x, Wv, bv, v_cache, o
                 nc.vector.memset(e_t[:, T + (i + 1) * P :], 0.0)
             e_sb.append(e_t)
 
-        def turn_words(rows, grouped):
+        def turn_words(rows, grouped, second_copy):
             for pair in range(2):
                 planes = psum_turn.tile([P, 4, P], F32, tag="turn")
                 for r in range(2):
@@ -107,17 +114,15 @@ def tile_attentionlayer_pa_t_kernel(tc, q, k_cache, k_new, x, Wv, bv, v_cache, o
                     for u in range(2):
                         nc.tensor.transpose(out=planes[:, 2 * r + u, :], in_=words[:, u * P : (u + 1) * P], identity=ident_f32[:])
                 half = grouped[:, pair * 2 * P * PACK : (pair + 1) * 2 * P * PACK].bitcast(F32)
-                copy = nc.scalar.copy if pair == 0 else nc.vector.tensor_copy
+                copy = nc.scalar.copy if pair == 0 else second_copy
                 copy(
                     out=half.rearrange("p (r c u) -> p r c u", r=2, u=2),
                     in_=planes[:].rearrange("p (r u) c -> p r c u", u=2),
                 )
 
         w_grouped = const.tile([P, DIM * PACK], BF16, align_bytes=64)
-        turn_words(w_sb, w_grouped)
         w_codes = const.tile([P, DIM], U32, align_bytes=64)
         w_scales = const.tile([P, DIM], U8, align_bytes=64)
-        nc.vector.quantize_mx(out=w_codes[:].bitcast(FP8X4), scales=w_scales[:], in_=w_grouped[:])
 
         x_grouped, x_codes, x_scales, v_new, v_grouped, v_codes, v_scales = {}, {}, {}, {}, {}, {}, {}
 
@@ -129,7 +134,7 @@ def tile_attentionlayer_pa_t_kernel(tc, q, k_cache, k_new, x, Wv, bv, v_cache, o
 
         def turn_x(b):
             xg = values.tile([P, S * PACK], BF16, tag="xg", align_bytes=64)
-            turn_words(x_sb[b], xg)
+            turn_words(x_sb[b], xg, nc.vector.tensor_copy if b == 0 else nc.scalar.copy)
             x_grouped[b] = xg
 
         def regroup_v_cache(b, h):
@@ -179,18 +184,21 @@ def tile_attentionlayer_pa_t_kernel(tc, q, k_cache, k_new, x, Wv, bv, v_cache, o
                 v_scales[b].append(vs)
 
         def prepare_values(b, step):
+            heads_per_step = 2 if b == 0 else 1
+            new_from = 2 + TILES
             if step == 0:
                 turn_x(b)
             elif step == 1:
                 quantise_x(b)
-            elif step < 2 + TILES:
+            elif step < new_from:
                 project(b, step - 2)
-            elif step == 7 + TILES:
+            elif step == new_from + (2 if b == 0 else 5):
                 quantise_v(b)
-            if 1 <= step < 1 + H:
-                regroup_v_cache(b, step - 1)
-            elif 2 + TILES <= step < 2 + TILES + H:
-                regroup_v_new(b, step - 2 - TILES)
+            for h in range(H):
+                if step == 1 + h // heads_per_step:
+                    regroup_v_cache(b, h)
+                elif step == new_from + h // heads_per_step:
+                    regroup_v_new(b, h)
 
         turned, dT, score_banks, neg_scores, first_min, neg_max, row_sums, inverses = {}, {}, {}, {}, {}, {}, {}, {}
         e_turned, e_grouped, e_codes, e_scales, ctx_acc = {}, {}, {}, {}, {}
@@ -311,9 +319,10 @@ def tile_attentionlayer_pa_t_kernel(tc, q, k_cache, k_new, x, Wv, bv, v_cache, o
             return 0 <= n < STEPS
 
         stack.enter_context(tc.manual_schedule())
-        for j in range(-VALUES_AHEAD, STEPS + FINISH_BEHIND):
+        for j in range(-PREPARE_AHEAD, STEPS + FINISH_BEHIND):
             if in_range(j) and j % STEPS_PER_BATCH == 0 and j // STEPS_PER_BATCH + 2 < B:
-                load_values(j // STEPS_PER_BATCH + 2)
+                load_x(j // STEPS_PER_BATCH + 2)
+                load_v_cache(j // STEPS_PER_BATCH + 2)
             if in_range(j + HEADS_LOADED_AHEAD * TILES) and j >= 0 and j % TILES == 0:
                 load_head(j // TILES + HEADS_LOADED_AHEAD)
             if in_range(j):
@@ -341,6 +350,12 @@ def tile_attentionlayer_pa_t_kernel(tc, q, k_cache, k_new, x, Wv, bv, v_cache, o
                 copy_e(j - TRANSPOSE_BEHIND)
             if in_range(j + PREPARE_AHEAD):
                 prepare_copy(j + PREPARE_AHEAD)
+            if j == -FIRST_VALUES_AHEAD - 1:
+                turn_words(w_sb, w_grouped, nc.vector.tensor_copy)
+            elif j == -FIRST_VALUES_AHEAD + 1:
+                nc.vector.quantize_mx(out=w_codes[:].bitcast(FP8X4), scales=w_scales[:], in_=w_grouped[:])
+            if -FIRST_VALUES_AHEAD <= j < STEPS_PER_BATCH - VALUES_AHEAD:
+                prepare_values(0, j + FIRST_VALUES_AHEAD)
             b_next, step = divmod(j + VALUES_AHEAD, STEPS_PER_BATCH)
-            if b_next < B:
+            if 0 < b_next < B:
                 prepare_values(b_next, step)

@@ -20,6 +20,7 @@ TILES = S // P
 STEPS = B * H * TILES
 STEPS_PER_BATCH = H * TILES
 SCALE = 1.0 / math.sqrt(D)
+REGROUP = 32
 MASKED = -1.0e30
 
 FLOPS = 2 * B * H * S * (T + S) * D * 2 + 2 * B * S * DIM * DIM
@@ -49,6 +50,8 @@ def tile_attentionlayer_pa_t_kernel(tc, q, k_cache, k_new, x, Wv, bv, v_cache, o
         psum_scores = stack.enter_context(tc.psum_pool(name="psum_scores", bufs=4))
         psum_turn = stack.enter_context(tc.psum_pool(name="psum_turn", bufs=3))
         psum_ctx = stack.enter_context(tc.psum_pool(name="psum_ctx", bufs=1))
+
+        stack.enter_context(tc.manual_schedule())
 
         q_sb, kc_sb, kn_sb, x_sb, vc_sb = {}, {}, {}, {}, {}
 
@@ -98,7 +101,8 @@ def tile_attentionlayer_pa_t_kernel(tc, q, k_cache, k_new, x, Wv, bv, v_cache, o
         mask_bf = const.tile([P, P], BF16)
         nc.vector.tensor_copy(out=mask_bf[:], in_=mask_f32[:])
         bias = const.tile([P, DIM], F32)
-        nc.gpsimd.tensor_scalar(out=bias[:], in0=bias_bf[:], scalar1=1.0, scalar2=0.0, op0=ALU.mult, op1=ALU.add)
+        minus_one = const.tile([P, TILES], F32)
+        nc.gpsimd.memset(minus_one[:], -1.0)
         e_sb = []
         for i in range(TILES):
             e_t = const.tile([P, T + S], BF16, name="e%d" % i)
@@ -127,10 +131,12 @@ def tile_attentionlayer_pa_t_kernel(tc, q, k_cache, k_new, x, Wv, bv, v_cache, o
         x_grouped, x_codes, x_scales, v_new, v_grouped, v_codes, v_scales = {}, {}, {}, {}, {}, {}, {}
 
         def regroup(grouped, rows, h):
-            nc.gpsimd.tensor_scalar(
-                out=grouped[:, h * D * PACK : (h + 1) * D * PACK].rearrange("p (d t) -> p d t", t=PACK),
-                in0=rows, scalar1=1.0, scalar2=0.0, op0=ALU.mult, op1=ALU.add,
-            )
+            to = grouped[:, h * D * PACK : (h + 1) * D * PACK].rearrange("p (d t) -> p d t", t=PACK)
+            for d in range(0, D, REGROUP):
+                nc.gpsimd.tensor_scalar(
+                    out=to[:, d : d + REGROUP, :], in0=rows[:, d : d + REGROUP, :],
+                    scalar1=1.0, scalar2=0.0, op0=ALU.mult, op1=ALU.add,
+                )
 
         def turn_x(b):
             xg = values.tile([P, S * PACK], BF16, tag="xg", align_bytes=64)
@@ -304,7 +310,7 @@ def tile_attentionlayer_pa_t_kernel(tc, q, k_cache, k_new, x, Wv, bv, v_cache, o
 
         def invert_sums(head):
             inverse = small.tile([P, TILES], F32, tag="inverse")
-            nc.vector.reciprocal(out=inverse[:], in_=row_sums[head][:])
+            nc.gpsimd.tensor_tensor(out=inverse[:], in0=row_sums[head][:], in1=minus_one[:], op=ALU.pow)
             inverses[head] = inverse
 
         def finish_head(head):
@@ -318,7 +324,6 @@ def tile_attentionlayer_pa_t_kernel(tc, q, k_cache, k_new, x, Wv, bv, v_cache, o
         def in_range(n):
             return 0 <= n < STEPS
 
-        stack.enter_context(tc.manual_schedule())
         for j in range(-PREPARE_AHEAD, STEPS + FINISH_BEHIND):
             if in_range(j) and j % STEPS_PER_BATCH == 0 and j // STEPS_PER_BATCH + 2 < B:
                 load_x(j // STEPS_PER_BATCH + 2)
@@ -351,6 +356,7 @@ def tile_attentionlayer_pa_t_kernel(tc, q, k_cache, k_new, x, Wv, bv, v_cache, o
             if in_range(j + PREPARE_AHEAD):
                 prepare_copy(j + PREPARE_AHEAD)
             if j == -FIRST_VALUES_AHEAD - 1:
+                nc.gpsimd.tensor_scalar(out=bias[:], in0=bias_bf[:], scalar1=1.0, scalar2=0.0, op0=ALU.mult, op1=ALU.add)
                 turn_words(w_sb, w_grouped, nc.vector.tensor_copy)
             elif j == -FIRST_VALUES_AHEAD + 1:
                 nc.vector.quantize_mx(out=w_codes[:].bitcast(FP8X4), scales=w_scales[:], in_=w_grouped[:])

@@ -19,6 +19,7 @@ D = DIM // H
 TILES = S // P
 STEPS = B * H * TILES
 STEPS_PER_BATCH = H * TILES
+LAST_HEAD = B * H - 1
 SCALE = 1.0 / math.sqrt(D)
 REGROUP = 32
 MASKED = -1.0e30
@@ -109,6 +110,7 @@ def tile_attentionlayer_pa_t_kernel(tc, q, k_cache, k_new, x, Wv, bv, v_cache, o
             if i + 1 < TILES:
                 nc.vector.memset(e_t[:, T + (i + 1) * P :], 0.0)
             e_sb.append(e_t)
+        e_last = const.tile([P, T + S], BF16)
 
         def turn_words(rows, grouped, second_copy):
             for pair in range(2):
@@ -209,6 +211,14 @@ def tile_attentionlayer_pa_t_kernel(tc, q, k_cache, k_new, x, Wv, bv, v_cache, o
         turned, dT, score_banks, neg_scores, first_min, neg_max, row_sums, inverses = {}, {}, {}, {}, {}, {}, {}, {}
         e_turned, e_grouped, e_codes, e_scales, ctx_acc = {}, {}, {}, {}, {}
 
+        def locate(n):
+            head, r = divmod(n, TILES)
+            return head, (TILES - 1 - r if head == LAST_HEAD else r)
+
+        def e_tile(n):
+            head, i = locate(n)
+            return e_last if head == LAST_HEAD and i == TILES - 1 else e_sb[i]
+
         def prepare_transposes(n):
             head, r = divmod(n, TILES)
             if r < 3:
@@ -227,13 +237,13 @@ def tile_attentionlayer_pa_t_kernel(tc, q, k_cache, k_new, x, Wv, bv, v_cache, o
                 nc.scalar.copy(out=dT[head][:, r, :], in_=turned[n][:].rearrange("p t c -> p (t c)"))
 
         def scores_cache(n):
-            head, i = divmod(n, TILES)
+            head, i = locate(n)
             cache = psum_scores.tile([P, T], F32, tag="scores")
             nc.tensor.matmul(out=cache[:], lhsT=dT[head][:, 0, i * P : (i + 1) * P], rhs=dT[head][:, 1, :], start=True, stop=True)
             score_banks[n] = [cache[:]]
 
         def scores_new(n):
-            head, i = divmod(n, TILES)
+            head, i = locate(n)
             qT = dT[head][:, 0, i * P : (i + 1) * P]
             seen = (i + 1) * P
             new = psum_scores.tile([P, S], F32, tag="scores")
@@ -251,7 +261,7 @@ def tile_attentionlayer_pa_t_kernel(tc, q, k_cache, k_new, x, Wv, bv, v_cache, o
             neg_scores[n], first_min[n] = neg_s, first
 
         def row_max_new(n):
-            seen = (n % TILES + 1) * P
+            seen = (locate(n)[1] + 1) * P
             nm = small.tile([P, 1], F32, tag="nm")
             nc.vector.tensor_scalar(
                 out=neg_scores[n][:, T : T + seen], in0=score_banks[n][1], scalar1=-SCALE, scalar2=first_min[n][:],
@@ -260,20 +270,19 @@ def tile_attentionlayer_pa_t_kernel(tc, q, k_cache, k_new, x, Wv, bv, v_cache, o
             neg_max[n] = nm
 
         def exponentials(n):
-            head, i = divmod(n, TILES)
-            if i == 0:
+            head, i = locate(n)
+            if n % TILES == 0:
                 sums = small.tile([P, TILES], F32, tag="sums")
                 row_sums[head] = sums
             keys = T + (i + 1) * P
             nc.scalar.activation(
-                out=e_sb[i][:, :keys], in_=neg_scores[n][:, :keys], func=ACT.Exp,
+                out=e_tile(n)[:, :keys], in_=neg_scores[n][:, :keys], func=ACT.Exp,
                 bias=neg_max[n][:], scale=-1.0, accum_out=row_sums[head][:, i : i + 1],
             )
 
         def transpose_e(n):
-            i = n % TILES
             blocks = psum_turn.tile([P, PACK, P], F32, tag="turn")
-            words = e_sb[i][:].bitcast(F32)
+            words = e_tile(n)[:].bitcast(F32)
             for t in range(PACK):
                 nc.tensor.transpose(out=blocks[:, t, :], in_=words[:, t * P : (t + 1) * P], identity=ident_f32[:])
             e_turned[n] = blocks
@@ -292,34 +301,54 @@ def tile_attentionlayer_pa_t_kernel(tc, q, k_cache, k_new, x, Wv, bv, v_cache, o
             nc.vector.quantize_mx(out=ec[:].bitcast(FP8X4), scales=es[:], in_=e_grouped[n][:])
             e_codes[n], e_scales[n] = ec, es
 
-        def attend(head):
-            b, h = divmod(head, H)
-            acc = psum_ctx.tile([P, TILES, D], F32, tag="ctx")
-            for i in range(TILES):
-                n = head * TILES + i
+        def attend(steps):
+            for n in steps:
+                head, i = locate(n)
+                b, h = divmod(head, H)
+                if head == LAST_HEAD:
+                    acc = psum_turn.tile([P, TILES, D], F32, tag="turn")
+                    ctx_acc[head] = acc
+                elif n % TILES == 0:
+                    acc = psum_ctx.tile([P, TILES, D], F32, tag="ctx")
+                    ctx_acc[head] = acc
                 for g in range(2):
                     nc.tensor.matmul_mx(
-                        out=acc[:, i, :],
+                        out=ctx_acc[head][:, i, :],
                         lhsT=e_codes[n][:, g * P : (g + 1) * P].bitcast(FP8X4),
                         lhsT_scale=e_scales[n][:, g * P : (g + 1) * P],
                         rhs=v_codes[b][g][:, h * D : (h + 1) * D].bitcast(FP8X4),
                         rhs_scale=v_scales[b][g][:, h * D : (h + 1) * D],
                         start=(g == 0), stop=(g == 1),
                     )
-            ctx_acc[head] = acc
 
-        def invert_sums(head):
+        def invert_sums(head, tiles):
             inverse = small.tile([P, TILES], F32, tag="inverse")
-            nc.gpsimd.tensor_tensor(out=inverse[:], in0=row_sums[head][:], in1=minus_one[:], op=ALU.pow)
+            if head == LAST_HEAD:
+                nc.vector.reciprocal(out=inverse[:, tiles], in_=row_sums[head][:, tiles])
+            else:
+                nc.gpsimd.tensor_tensor(out=inverse[:], in0=row_sums[head][:], in1=minus_one[:], op=ALU.pow)
             inverses[head] = inverse
 
-        def finish_head(head):
+        def finish(head, tiles):
             b, h = divmod(head, H)
-            ctx = work.tile([P, TILES, D], F32, tag="ctx")
+            count = tiles.stop - tiles.start
+            ctx = work.tile([P, count, D], F32, tag="ctx")
             nc.vector.tensor_tensor(
-                out=ctx[:], in0=ctx_acc[head][:], in1=inverses[head][:].unsqueeze(2).to_broadcast([P, TILES, D]), op=ALU.mult
+                out=ctx[:], in0=ctx_acc[head][:, tiles, :],
+                in1=inverses[head][:, tiles].unsqueeze(2).to_broadcast([P, count, D]), op=ALU.mult,
             )
-            nc.sync.dma_start(out=out_0[b, :, h * D : (h + 1) * D].rearrange("(i p) d -> p i d", p=P), in_=ctx[:])
+            rows = out_0[b, tiles.start * P : tiles.stop * P, h * D : (h + 1) * D]
+            nc.sync.dma_start(out=rows.rearrange("(i p) d -> p i d", p=P), in_=ctx[:])
+
+        def ready(n):
+            if not in_range(n):
+                return None
+            head, i = locate(n)
+            if head == LAST_HEAD:
+                return head, [n], slice(i, i + 1)
+            if n % TILES == TILES - 1:
+                return head, range(n + 1 - TILES, n + 1), slice(0, TILES)
+            return None
 
         def in_range(n):
             return 0 <= n < STEPS
@@ -332,25 +361,27 @@ def tile_attentionlayer_pa_t_kernel(tc, q, k_cache, k_new, x, Wv, bv, v_cache, o
                 load_head(j // TILES + HEADS_LOADED_AHEAD)
             if in_range(j):
                 exponentials(j)
+            if in_range(j + SCORES_AHEAD):
+                scores_cache(j + SCORES_AHEAD)
             if in_range(j - TRANSPOSE_BEHIND):
                 transpose_e(j - TRANSPOSE_BEHIND)
             if in_range(j - QUANTISE_BEHIND):
                 quantise_e(j - QUANTISE_BEHIND)
-            if in_range(j + SCORES_AHEAD):
-                scores_cache(j + SCORES_AHEAD)
             if in_range(j + PREPARE_AHEAD):
                 prepare_transposes(j + PREPARE_AHEAD)
             if in_range(j + SCORES_AHEAD):
                 scores_new(j + SCORES_AHEAD)
             if in_range(j + MAX_AHEAD):
                 row_max_new(j + MAX_AHEAD)
-            if in_range(j - FINISH_BEHIND) and (j - FINISH_BEHIND) % TILES == TILES - 1:
-                finish_head((j - FINISH_BEHIND) // TILES)
+            done = ready(j - FINISH_BEHIND)
+            if done:
+                finish(done[0], done[2])
             if in_range(j + MAX_AHEAD + 1):
                 row_max_cache(j + MAX_AHEAD + 1)
-            if in_range(j - ATTEND_BEHIND) and (j - ATTEND_BEHIND) % TILES == TILES - 1:
-                invert_sums((j - ATTEND_BEHIND) // TILES)
-                attend((j - ATTEND_BEHIND) // TILES)
+            done = ready(j - ATTEND_BEHIND)
+            if done:
+                invert_sums(done[0], done[2])
+                attend(done[1])
             if in_range(j - TRANSPOSE_BEHIND):
                 copy_e(j - TRANSPOSE_BEHIND)
             if in_range(j + PREPARE_AHEAD):

@@ -27,8 +27,11 @@ MASKED = -1.0e30
 FLOPS = 2 * B * H * S * (T + S) * D * 2 + 2 * B * S * DIM * DIM
 
 PREPARE_AHEAD = 7
-SCORES_AHEAD = 3
-MAX_AHEAD = 2
+CACHE_SCORES_AHEAD = 4
+CACHE_MAX_AHEAD = 3
+NEW_SCORES_AHEAD = 2
+NEW_MAX_AHEAD = 2
+SCORE_BANKS = 4
 TRANSPOSE_BEHIND = 1
 QUANTISE_BEHIND = 2
 ATTEND_BEHIND = 3
@@ -48,7 +51,7 @@ def tile_attentionlayer_pa_t_kernel(tc, q, k_cache, k_new, x, Wv, bv, v_cache, o
         work = stack.enter_context(tc.tile_pool(name="work", bufs=3))
         codes = stack.enter_context(tc.tile_pool(name="codes", bufs=2 * TILES))
         values = stack.enter_context(tc.tile_pool(name="values", bufs=2))
-        psum_scores = stack.enter_context(tc.psum_pool(name="psum_scores", bufs=4))
+        psum_scores = stack.enter_context(tc.psum_pool(name="psum_scores", bufs=1))
         psum_turn = stack.enter_context(tc.psum_pool(name="psum_turn", bufs=3))
         psum_ctx = stack.enter_context(tc.psum_pool(name="psum_ctx", bufs=1))
 
@@ -238,7 +241,7 @@ def tile_attentionlayer_pa_t_kernel(tc, q, k_cache, k_new, x, Wv, bv, v_cache, o
 
         def scores_cache(n):
             head, i = locate(n)
-            cache = psum_scores.tile([P, T], F32, tag="scores")
+            cache = psum_scores.tile([P, T], F32, tag="scores%d" % (n % SCORE_BANKS))
             nc.tensor.matmul(out=cache[:], lhsT=dT[head][:, 0, i * P : (i + 1) * P], rhs=dT[head][:, 1, :], start=True, stop=True)
             score_banks[n] = [cache[:]]
 
@@ -246,13 +249,13 @@ def tile_attentionlayer_pa_t_kernel(tc, q, k_cache, k_new, x, Wv, bv, v_cache, o
             head, i = locate(n)
             qT = dT[head][:, 0, i * P : (i + 1) * P]
             seen = (i + 1) * P
-            new = psum_scores.tile([P, S], F32, tag="scores")
+            new = psum_scores.tile([P, S], F32, tag="scores%d" % (n % SCORE_BANKS))
             nc.tensor.matmul(out=new[:], lhsT=qT, rhs=dT[head][:, 2, :], start=True, stop=False)
             nc.tensor.matmul(out=new[:, i * P : seen], lhsT=ident_bf[:], rhs=mask_bf[:], start=False, stop=True)
             score_banks[n].append(new[:, :seen])
 
         def row_max_cache(n):
-            neg_s = work.tile([P, T + S], F32, tag="neg_s", bufs=4)
+            neg_s = work.tile([P, T + S], F32, tag="neg_s", bufs=5)
             first = small.tile([P, 1], F32, tag="first")
             nc.vector.tensor_scalar(
                 out=neg_s[:, :T], in0=score_banks[n][0], scalar1=-SCALE, scalar2=None,
@@ -359,25 +362,25 @@ def tile_attentionlayer_pa_t_kernel(tc, q, k_cache, k_new, x, Wv, bv, v_cache, o
                 load_v_cache(j // STEPS_PER_BATCH + 2)
             if in_range(j + HEADS_LOADED_AHEAD * TILES) and j >= 0 and j % TILES == 0:
                 load_head(j // TILES + HEADS_LOADED_AHEAD)
+            if in_range(j + CACHE_MAX_AHEAD):
+                row_max_cache(j + CACHE_MAX_AHEAD)
             if in_range(j):
                 exponentials(j)
-            if in_range(j + SCORES_AHEAD):
-                scores_cache(j + SCORES_AHEAD)
             if in_range(j - TRANSPOSE_BEHIND):
                 transpose_e(j - TRANSPOSE_BEHIND)
-            if in_range(j - QUANTISE_BEHIND):
-                quantise_e(j - QUANTISE_BEHIND)
             if in_range(j + PREPARE_AHEAD):
                 prepare_transposes(j + PREPARE_AHEAD)
-            if in_range(j + SCORES_AHEAD):
-                scores_new(j + SCORES_AHEAD)
-            if in_range(j + MAX_AHEAD):
-                row_max_new(j + MAX_AHEAD)
+            if in_range(j + NEW_SCORES_AHEAD):
+                scores_new(j + NEW_SCORES_AHEAD)
+            if in_range(j + CACHE_SCORES_AHEAD):
+                scores_cache(j + CACHE_SCORES_AHEAD)
+            if in_range(j - QUANTISE_BEHIND):
+                quantise_e(j - QUANTISE_BEHIND)
             done = ready(j - FINISH_BEHIND)
             if done:
                 finish(done[0], done[2])
-            if in_range(j + MAX_AHEAD + 1):
-                row_max_cache(j + MAX_AHEAD + 1)
+            if in_range(j + NEW_MAX_AHEAD):
+                row_max_new(j + NEW_MAX_AHEAD)
             done = ready(j - ATTEND_BEHIND)
             if done:
                 invert_sums(done[0], done[2])

import math
from contextlib import ExitStack

import concourse.mybir as mybir
from concourse.masks import make_identity

F32 = mybir.dt.float32
BF16 = mybir.dt.bfloat16
U32 = mybir.dt.uint32
U8 = mybir.dt.uint8
FP8X4 = mybir.dt.float8_e4m3fn_x4
ALU = mybir.AluOpType
ACT = mybir.ActivationFunctionType

P = 128
PACK = 4
B, H, S, T, DIM = 8, 4, 512, 512, 512
D = DIM // H
TILES = S // P
STEPS = B * H * TILES
STEPS_PER_BATCH = H * TILES
LAST_HEAD = B * H - 1
SCALE = 1.0 / math.sqrt(D)
REGROUP = 32
MASKED = -1.0e30

FLOPS = 2 * B * H * S * (T + S) * D * 2 + 2 * B * S * DIM * DIM

PREPARE_AHEAD = 7
CACHE_SCORES_AHEAD = 4
CACHE_MAX_AHEAD = 3
NEW_SCORES_AHEAD = 2
NEW_MAX_AHEAD = 2
SCORE_BANKS = 4
TRANSPOSE_BEHIND = 1
QUANTISE_BEHIND = 2
ATTEND_BEHIND = 3
FINISH_BEHIND = 4
HEADS_LOADED_AHEAD = 4
VALUES_AHEAD = 7
FIRST_VALUES_AHEAD = 3


def tile_attentionlayer_pa_t_kernel(tc, q, k_cache, k_new, x, Wv, bv, v_cache, out_0, out_1):
    nc = tc.nc
    with ExitStack() as stack:
        const = stack.enter_context(tc.tile_pool(name="const", bufs=1))
        loads = stack.enter_context(tc.tile_pool(name="loads", bufs=3))
        heads = stack.enter_context(tc.tile_pool(name="heads", bufs=3))
        small = stack.enter_context(tc.tile_pool(name="small", bufs=6))
        work = stack.enter_context(tc.tile_pool(name="work", bufs=3))
        codes = stack.enter_context(tc.tile_pool(name="codes", bufs=2 * TILES))
        values = stack.enter_context(tc.tile_pool(name="values", bufs=2))
        psum_scores = stack.enter_context(tc.psum_pool(name="psum_scores", bufs=1))
        psum_turn = stack.enter_context(tc.psum_pool(name="psum_turn", bufs=3))
        psum_ctx = stack.enter_context(tc.psum_pool(name="psum_ctx", bufs=1))

        stack.enter_context(tc.manual_schedule())

        q_sb, kc_sb, kn_sb, x_sb, vc_sb = {}, {}, {}, {}, {}

        def load_head(head):
            b, h = divmod(head, H)
            q_t = loads.tile([P, TILES, D], BF16, tag="q", bufs=HEADS_LOADED_AHEAD + 2)
            nc.sync.dma_start(out=q_t[:], in_=q[b, h].rearrange("(i p) d -> p i d", p=P))
            kc_t = loads.tile([P, TILES, D], BF16, tag="kc", bufs=HEADS_LOADED_AHEAD + 2)
            nc.sync.dma_start(out=kc_t[:], in_=k_cache[b, h].rearrange("(t p) d -> p t d", p=P))
            kn_t = loads.tile([P, TILES, D], BF16, tag="kn", bufs=HEADS_LOADED_AHEAD + 2)
            nc.sync.dma_start(out=kn_t[:], in_=k_new[b, h].rearrange("(t p) d -> p t d", p=P))
            q_sb[head], kc_sb[head], kn_sb[head] = q_t, kc_t, kn_t

        def load_x(b):
            x_t = loads.tile([P, TILES, DIM], BF16, tag="x")
            nc.sync.dma_start(out=x_t[:].rearrange("p (u e) f -> p u (e f)", e=2), in_=x[b].rearrange("(u p e) f -> p u (e f)", p=P, e=2))
            x_sb[b] = x_t

        def load_v_cache(b):
            vc_t = loads.tile([P, H, PACK * D], BF16, tag="vc")
            nc.sync.dma_start(out=vc_t[:].rearrange("p h (u r) -> p (h u) r", u=2), in_=v_cache[b].rearrange("h (u p e) d -> p (h u) (e d)", p=P, e=2))
            vc_sb[b] = vc_t

        load_head(0)
        w_sb = const.tile([P, TILES, DIM], BF16)
        nc.sync.dma_start(out=w_sb[:], in_=Wv.rearrange("(r p) k -> p r k", p=P))
        load_x(0)
        load_head(1)
        bias_bf = const.tile([P, DIM], BF16)
        nc.sync.dma_start(out=bias_bf[:], in_=bv.partition_broadcast(P))
        load_v_cache(0)
        for head in range(2, HEADS_LOADED_AHEAD):
            load_head(head)
        load_x(1)
        load_v_cache(1)

        ident_bf = const.tile([P, P], BF16)
        make_identity(nc, ident_bf[:])
        ident_f32 = const.tile([P, P], F32)
        make_identity(nc, ident_f32[:])
        mask_f32 = const.tile([P, P], F32)
        nc.gpsimd.memset(mask_f32[:], 0.0)
        nc.gpsimd.affine_select(
            out=mask_f32[:], in_=mask_f32[:], compare_op=ALU.is_ge, fill=MASKED,
            base=0, pattern=[[-1, P]], channel_multiplier=1,
        )
        mask_bf = const.tile([P, P], BF16)
        nc.vector.tensor_copy(out=mask_bf[:], in_=mask_f32[:])
        bias = const.tile([P, DIM], F32)
        minus_one = const.tile([P, TILES], F32)
        nc.gpsimd.memset(minus_one[:], -1.0)
        e_sb = []
        for i in range(TILES):
            e_t = const.tile([P, T + S], BF16, name="e%d" % i)
            if i + 1 < TILES:
                nc.vector.memset(e_t[:, T + (i + 1) * P :], 0.0)
            e_sb.append(e_t)
        e_last = const.tile([P, T + S], BF16)

        def turn_words(rows, grouped, second_copy):
            for pair in range(2):
                planes = psum_turn.tile([P, 4, P], F32, tag="turn")
                for r in range(2):
                    words = rows[:, 2 * pair + r, :].bitcast(F32)
                    for u in range(2):
                        nc.tensor.transpose(out=planes[:, 2 * r + u, :], in_=words[:, u * P : (u + 1) * P], identity=ident_f32[:])
                half = grouped[:, pair * 2 * P * PACK : (pair + 1) * 2 * P * PACK].bitcast(F32)
                copy = nc.scalar.copy if pair == 0 else second_copy
                copy(
                    out=half.rearrange("p (r c u) -> p r c u", r=2, u=2),
                    in_=planes[:].rearrange("p (r u) c -> p r c u", u=2),
                )

        w_grouped = const.tile([P, DIM * PACK], BF16, align_bytes=64)
        w_codes = const.tile([P, DIM], U32, align_bytes=64)
        w_scales = const.tile([P, DIM], U8, align_bytes=64)

        x_grouped, x_codes, x_scales, v_new, v_grouped, v_codes, v_scales = {}, {}, {}, {}, {}, {}, {}

        def regroup(grouped, rows, h):
            to = grouped[:, h * D * PACK : (h + 1) * D * PACK].rearrange("p (d t) -> p d t", t=PACK)
            for d in range(0, D, REGROUP):
                nc.gpsimd.tensor_scalar(
                    out=to[:, d : d + REGROUP, :], in0=rows[:, d : d + REGROUP, :],
                    scalar1=1.0, scalar2=0.0, op0=ALU.mult, op1=ALU.add,
                )

        def turn_x(b):
            xg = values.tile([P, S * PACK], BF16, tag="xg", align_bytes=64)
            turn_words(x_sb[b], xg, nc.vector.tensor_copy if b == 0 else nc.scalar.copy)
            x_grouped[b] = xg

        def regroup_v_cache(b, h):
            if h == 0:
                vg_cache = values.tile([P, DIM * PACK], BF16, tag="vg_cache", align_bytes=64)
                v_grouped[b] = [vg_cache]
            regroup(v_grouped[b][0], vc_sb[b][:, h, :].rearrange("p (t d) -> p d t", t=PACK), h)

        def quantise_x(b):
            xc = values.tile([P, S], U32, tag="xc", align_bytes=64)
            xs = values.tile([P, S], U8, tag="xs", align_bytes=64)
            nc.vector.quantize_mx(out=xc[:].bitcast(FP8X4), scales=xs[:], in_=x_grouped[b][:])
            x_codes[b], x_scales[b] = xc, xs
            vn = values.tile([P, H, TILES, D], F32, tag="vn")
            v_new[b] = vn

        def project(b, t):
            cols = slice(t * P, (t + 1) * P)
            acc = psum_turn.tile([P, DIM], F32, tag="turn")
            nc.tensor.matmul_mx(
                out=acc[:],
                lhsT=x_codes[b][:, cols].bitcast(FP8X4), lhsT_scale=x_scales[b][:, cols],
                rhs=w_codes[:].bitcast(FP8X4), rhs_scale=w_scales[:],
                start=True, stop=True,
            )
            nc.vector.tensor_tensor(
                out=v_new[b][:, :, t, :],
                in0=acc[:].rearrange("p (h d) -> p h d", h=H),
                in1=bias[:].rearrange("p (h d) -> p h d", h=H),
                op=ALU.add,
            )

        def regroup_v_new(b, h):
            if h == 0:
                nc.sync.dma_start(out=out_1[b].rearrange("h (u p e) d -> p (h u) (e d)", p=P, e=2), in_=v_new[b][:].rearrange("p h (u e) d -> p (h u) (e d)", e=2))
                vg_new = values.tile([P, DIM * PACK], BF16, tag="vg_new", align_bytes=64)
                v_grouped[b].append(vg_new)
            regroup(v_grouped[b][1], v_new[b][:, h, :, :].rearrange("p t d -> p d t"), h)

        def quantise_v(b):
            v_codes[b], v_scales[b] = [], []
            for g in range(2):
                vc = values.tile([P, DIM], U32, tag="vc%d" % g, align_bytes=64)
                vs = values.tile([P, DIM], U8, tag="vs%d" % g, align_bytes=64)
                nc.vector.quantize_mx(out=vc[:].bitcast(FP8X4), scales=vs[:], in_=v_grouped[b][g][:])
                v_codes[b].append(vc)
                v_scales[b].append(vs)

        def prepare_values(b, step):
            heads_per_step = 2 if b == 0 else 1
            new_from = 2 + TILES
            if step == 0:
                turn_x(b)
            elif step == 1:
                quantise_x(b)
            elif step < new_from:
                project(b, step - 2)
            elif step == new_from + (2 if b == 0 else 5):
                quantise_v(b)
            for h in range(H):
                if step == 1 + h // heads_per_step:
                    regroup_v_cache(b, h)
                elif step == new_from + h // heads_per_step:
                    regroup_v_new(b, h)

        turned, dT, score_banks, neg_scores, first_min, neg_max, row_sums, inverses = {}, {}, {}, {}, {}, {}, {}, {}
        e_turned, e_grouped, e_codes, e_scales, ctx_acc = {}, {}, {}, {}, {}

        def locate(n):
            head, r = divmod(n, TILES)
            return head, (TILES - 1 - r if head == LAST_HEAD else r)

        def e_tile(n):
            head, i = locate(n)
            return e_last if head == LAST_HEAD and i == TILES - 1 else e_sb[i]

        def prepare_transposes(n):
            head, r = divmod(n, TILES)
            if r < 3:
                rows = (q_sb, kc_sb, kn_sb)[r][head]
                blocks = psum_turn.tile([P, TILES, P], BF16, tag="turn")
                for t in range(TILES):
                    nc.tensor.transpose(out=blocks[:, t, :], in_=rows[:, t, :], identity=ident_bf[:])
                turned[n] = blocks

        def prepare_copy(n):
            head, r = divmod(n, TILES)
            if r == 0:
                qkT = heads.tile([P, 3, S], BF16, tag="qkT")
                dT[head] = qkT
            if r < 3:
                nc.scalar.copy(out=dT[head][:, r, :], in_=turned[n][:].rearrange("p t c -> p (t c)"))

        def scores_cache(n):
            head, i = locate(n)
            cache = psum_scores.tile([P, T], F32, tag="scores%d" % (n % SCORE_BANKS))
            nc.tensor.matmul(out=cache[:], lhsT=dT[head][:, 0, i * P : (i + 1) * P], rhs=dT[head][:, 1, :], start=True, stop=True)
            score_banks[n] = [cache[:]]

        def scores_new(n):
            head, i = locate(n)
            qT = dT[head][:, 0, i * P : (i + 1) * P]
            seen = (i + 1) * P
            new = psum_scores.tile([P, S], F32, tag="scores%d" % (n % SCORE_BANKS))
            nc.tensor.matmul(out=new[:], lhsT=qT, rhs=dT[head][:, 2, :], start=True, stop=False)
            nc.tensor.matmul(out=new[:, i * P : seen], lhsT=ident_bf[:], rhs=mask_bf[:], start=False, stop=True)
            score_banks[n].append(new[:, :seen])

        def row_max_cache(n):
            neg_s = work.tile([P, T + S], F32, tag="neg_s", bufs=5)
            first = small.tile([P, 1], F32, tag="first")
            nc.vector.tensor_scalar(
                out=neg_s[:, :T], in0=score_banks[n][0], scalar1=-SCALE, scalar2=None,
                op0=ALU.mult, op1=ALU.min, accum_out=first[:],
            )
            neg_scores[n], first_min[n] = neg_s, first

        def row_max_new(n):
            seen = (locate(n)[1] + 1) * P
            nm = small.tile([P, 1], F32, tag="nm")
            nc.vector.tensor_scalar(
                out=neg_scores[n][:, T : T + seen], in0=score_banks[n][1], scalar1=-SCALE, scalar2=first_min[n][:],
                op0=ALU.mult, op1=ALU.min, accum_out=nm[:],
            )
            neg_max[n] = nm

        def exponentials(n):
            head, i = locate(n)
            if n % TILES == 0:
                sums = small.tile([P, TILES], F32, tag="sums")
                row_sums[head] = sums
            keys = T + (i + 1) * P
            nc.scalar.activation(
                out=e_tile(n)[:, :keys], in_=neg_scores[n][:, :keys], func=ACT.Exp,
                bias=neg_max[n][:], scale=-1.0, accum_out=row_sums[head][:, i : i + 1],
            )

        def transpose_e(n):
            blocks = psum_turn.tile([P, PACK, P], F32, tag="turn")
            words = e_tile(n)[:].bitcast(F32)
            for t in range(PACK):
                nc.tensor.transpose(out=blocks[:, t, :], in_=words[:, t * P : (t + 1) * P], identity=ident_f32[:])
            e_turned[n] = blocks

        def copy_e(n):
            eg = work.tile([P, 2 * P * PACK], BF16, tag="eg", align_bytes=64)
            nc.scalar.copy(
                out=eg[:].bitcast(F32).rearrange("p (g c u) -> p g c u", g=2, u=2),
                in_=e_turned[n][:].rearrange("p (g u) c -> p g c u", g=2),
            )
            e_grouped[n] = eg

        def quantise_e(n):
            ec = codes.tile([P, 2 * P], U32, tag="ec", align_bytes=64)
            es = codes.tile([P, 2 * P], U8, tag="es", align_bytes=64)
            nc.vector.quantize_mx(out=ec[:].bitcast(FP8X4), scales=es[:], in_=e_grouped[n][:])
            e_codes[n], e_scales[n] = ec, es

        def attend(steps):
            for n in steps:
                head, i = locate(n)
                b, h = divmod(head, H)
                if head == LAST_HEAD:
                    acc = psum_turn.tile([P, TILES, D], F32, tag="turn")
                    ctx_acc[head] = acc
                elif n % TILES == 0:
                    acc = psum_ctx.tile([P, TILES, D], F32, tag="ctx")
                    ctx_acc[head] = acc
                for g in range(2):
                    nc.tensor.matmul_mx(
                        out=ctx_acc[head][:, i, :],
                        lhsT=e_codes[n][:, g * P : (g + 1) * P].bitcast(FP8X4),
                        lhsT_scale=e_scales[n][:, g * P : (g + 1) * P],
                        rhs=v_codes[b][g][:, h * D : (h + 1) * D].bitcast(FP8X4),
                        rhs_scale=v_scales[b][g][:, h * D : (h + 1) * D],
                        start=(g == 0), stop=(g == 1),
                    )

        def invert_sums(head, tiles):
            inverse = small.tile([P, TILES], F32, tag="inverse")
            if head == LAST_HEAD:
                nc.vector.reciprocal(out=inverse[:, tiles], in_=row_sums[head][:, tiles])
            else:
                nc.gpsimd.tensor_tensor(out=inverse[:], in0=row_sums[head][:], in1=minus_one[:], op=ALU.pow)
            inverses[head] = inverse

        def finish(head, tiles):
            b, h = divmod(head, H)
            count = tiles.stop - tiles.start
            ctx = work.tile([P, count, D], F32, tag="ctx")
            nc.vector.tensor_tensor(
                out=ctx[:], in0=ctx_acc[head][:, tiles, :],
                in1=inverses[head][:, tiles].unsqueeze(2).to_broadcast([P, count, D]), op=ALU.mult,
            )
            rows = out_0[b, tiles.start * P : tiles.stop * P, h * D : (h + 1) * D]
            nc.sync.dma_start(out=rows.rearrange("(i p) d -> p i d", p=P), in_=ctx[:])

        def ready(n):
            if not in_range(n):
                return None
            head, i = locate(n)
            if head == LAST_HEAD:
                return head, [n], slice(i, i + 1)
            if n % TILES == TILES - 1:
                return head, range(n + 1 - TILES, n + 1), slice(0, TILES)
            return None

        def in_range(n):
            return 0 <= n < STEPS

        for j in range(-PREPARE_AHEAD, STEPS + FINISH_BEHIND):
            if in_range(j) and j % STEPS_PER_BATCH == 0 and j // STEPS_PER_BATCH + 2 < B:
                load_x(j // STEPS_PER_BATCH + 2)
                load_v_cache(j // STEPS_PER_BATCH + 2)
            if in_range(j + HEADS_LOADED_AHEAD * TILES) and j >= 0 and j % TILES == 0:
                load_head(j // TILES + HEADS_LOADED_AHEAD)
            if in_range(j + CACHE_MAX_AHEAD):
                row_max_cache(j + CACHE_MAX_AHEAD)
            if in_range(j):
                exponentials(j)
            if in_range(j - TRANSPOSE_BEHIND):
                transpose_e(j - TRANSPOSE_BEHIND)
            if in_range(j + PREPARE_AHEAD):
                prepare_transposes(j + PREPARE_AHEAD)
            if in_range(j + NEW_SCORES_AHEAD):
                scores_new(j + NEW_SCORES_AHEAD)
            if in_range(j + CACHE_SCORES_AHEAD):
                scores_cache(j + CACHE_SCORES_AHEAD)
            if in_range(j - QUANTISE_BEHIND):
                quantise_e(j - QUANTISE_BEHIND)
            done = ready(j - FINISH_BEHIND)
            if done:
                finish(done[0], done[2])
            if in_range(j + NEW_MAX_AHEAD):
                row_max_new(j + NEW_MAX_AHEAD)
            done = ready(j - ATTEND_BEHIND)
            if done:
                invert_sums(done[0], done[2])
                attend(done[1])
            if in_range(j - TRANSPOSE_BEHIND):
                copy_e(j - TRANSPOSE_BEHIND)
            if in_range(j + PREPARE_AHEAD):
                prepare_copy(j + PREPARE_AHEAD)
            if j == -FIRST_VALUES_AHEAD - 1:
                nc.gpsimd.tensor_scalar(out=bias[:], in0=bias_bf[:], scalar1=1.0, scalar2=0.0, op0=ALU.mult, op1=ALU.add)
                turn_words(w_sb, w_grouped, nc.vector.tensor_copy)
            elif j == -FIRST_VALUES_AHEAD + 1:
                nc.vector.quantize_mx(out=w_codes[:].bitcast(FP8X4), scales=w_scales[:], in_=w_grouped[:])
            if -FIRST_VALUES_AHEAD <= j < STEPS_PER_BATCH - VALUES_AHEAD:
                prepare_values(0, j + FIRST_VALUES_AHEAD)
            b_next, step = divmod(j + VALUES_AHEAD, STEPS_PER_BATCH)
            if 0 < b_next < B:
                prepare_values(b_next, step)
